import numpy as np
import ml_dtypes


def mxq(x, axis, fmt="e4m3"):
    dtype, down = {"e4m3": (ml_dtypes.float8_e4m3fn, 7), "e5m2": (ml_dtypes.float8_e5m2, 14)}[fmt]
    v = np.moveaxis(np.asarray(x, np.float32).astype(ml_dtypes.bfloat16).astype(np.float64), axis, -1)
    blocks = v.reshape(v.shape[:-1] + (-1, 32))
    amax = np.abs(blocks).max(-1, keepdims=True)
    byte = np.maximum(np.where(amax > 0, np.frexp(amax)[1] - 1 + 127, 0) - down, 1)
    scale = np.exp2(byte - 127.0)
    codes = (blocks / scale).astype(np.float32).astype(dtype).astype(np.float64)
    return np.moveaxis((codes * scale).reshape(v.shape), -1, axis)


WIDE = False


def mx_kscale(k):
    if not WIDE:
        return np.ones(k)
    levels = np.array([10, -10, 5, -5, 0])
    if k % 512:
        return np.exp2(np.random.permutation(np.resize(levels, k // 32))).repeat(32)
    a = np.empty((k // 512, 16))
    for p in range(k // 512):
        a[p, :8] = np.random.permutation(np.resize(levels, 8))
        for g in range(8):
            far = levels[np.abs(levels - a[p, g]) >= 10]
            a[p, g + 8] = far[np.random.randint(len(far))]
    return np.exp2(a.ravel()).repeat(32)


BF16 = ml_dtypes.bfloat16


def bf(x):
    return np.asarray(x, np.float32).astype(BF16)


def f64(x):
    return np.asarray(x).astype(np.float64)


B, T, D, E, F = 4, 256, 1024, 1024, 4096
EPS = 1e-6


def rms_norm(x, w):
    rms = np.sqrt(np.mean(x * x, axis=-1, keepdims=True) + EPS)
    return x / rms * w


def setup_inputs():
    s = mx_kscale(D)
    return {"x": bf(np.random.standard_normal((B, T, D))),
            "attn_norm_w": bf((1.0 + 0.1 * np.random.standard_normal(D)) * s),
            "wq": bf(np.random.standard_normal((D, E)) * 1.5 / np.sqrt(D) / s[:, None]),
            "bq": bf(np.random.standard_normal(E) * 0.1),
            "wk": bf(np.random.standard_normal((D, E)) * 1.5 / np.sqrt(D) / s[:, None]),
            "bk": bf(np.random.standard_normal(E) * 0.1),
            "wv": bf(np.random.standard_normal((D, E)) / np.sqrt(D) / s[:, None]),
            "bv": bf(np.random.standard_normal(E) * 0.1)}


def reference(x, attn_norm_w, wq, bq, wk, bk, wv, bv):
    xn = mxq(rms_norm(f64(x), f64(attn_norm_w)), 2, "e4m3")
    q = (xn @ mxq(f64(wq), 0, "e4m3")) + f64(bq)
    k = (xn @ mxq(f64(wk), 0, "e4m3")) + f64(bk)
    v = (xn @ mxq(f64(wv), 0, "e4m3")) + f64(bv)
    return q, k, v

@@ -1,0 +1,245 @@
+from contextlib import ExitStack
+
+import concourse.mybir as mybir
+from concourse.masks import make_identity
+
+F32 = mybir.dt.float32
+BF16 = mybir.dt.bfloat16
+I32 = mybir.dt.int32
+U32 = mybir.dt.uint32
+U8 = mybir.dt.uint8
+FP8X4 = mybir.dt.float8_e4m3fn_x4
+ACT = mybir.ActivationFunctionType
+ALU = mybir.AluOpType
+
+P = 128
+PACK = 4
+K_PASS = P * PACK
+TOKENS = 4 * 256
+D = 1024
+E = 1024
+EPS = 1e-6
+PASSES = D // K_PASS
+TOK_TILES = TOKENS // P
+PAIRS = TOK_TILES // 2
+N_TILE = 512
+N_HALVES = E // N_TILE
+WEIGHTS = 3
+TILE_WORDS = PASSES * P
+
+LEAD = 2
+
+FLOPS = 2 * TOKENS * D * WEIGHTS * E
+
+assert PAIRS == 2 * LEAD
+assert PASSES == LEAD
+
+
+def tile_tinyblock_pa_kernel(
+    tc, x, attn_norm_w, wq, bq, wk, bk, wv, bv, out_0, out_1, out_2
+):
+    nc = tc.nc
+    weights = [wq, wk, wv]
+    vectors = [attn_norm_w, bq, bk, bv]
+    x_rows = x.flatten_outer_dims().rearrange("(p i) d -> p i d", i=TOK_TILES)
+    out_rows = [
+        o.flatten_outer_dims().rearrange("(p i) e -> p i e", i=TOK_TILES)
+        for o in (out_0, out_1, out_2)
+    ]
+
+    with ExitStack() as ctx:
+        ctx.enter_context(tc.manual_schedule())
+        keep = ctx.enter_context(tc.tile_pool(name="keep", bufs=1))
+        work = ctx.enter_context(tc.tile_pool(name="work", bufs=4))
+        results = ctx.enter_context(tc.tile_pool(name="results", bufs=6))
+        psum_stage = ctx.enter_context(tc.psum_pool(name="psum_stage", bufs=3))
+        psum_acc = ctx.enter_context(tc.psum_pool(name="psum_acc", bufs=5))
+
+        x_sb = keep.tile([P, TOK_TILES, D], BF16)
+        w_raw = [
+            [keep.tile([P, PACK, E], BF16, name="w_raw_%d_%d" % (w, c)) for c in range(PASSES)]
+            for w in range(WEIGHTS)
+        ]
+        x_codes = keep.tile([P, TOK_TILES * TILE_WORDS], U32, align_bytes=64)
+        x_scales = keep.tile([P, TOK_TILES * TILE_WORDS], U8, align_bytes=64)
+        w_codes = [
+            keep.tile([P, PASSES, E], U32, name="w_codes_%d" % w, align_bytes=64)
+            for w in range(WEIGHTS)
+        ]
+        w_scales = [
+            keep.tile([P, PASSES, E], U8, name="w_scales_%d" % w, align_bytes=64)
+            for w in range(WEIGHTS)
+        ]
+        vec_rows = keep.tile([P, 1 + WEIGHTS, E], BF16)
+        vec_all = keep.tile([P, 1 + WEIGHTS, E], BF16)
+        ones = keep.tile([P, P], BF16)
+        ident = keep.tile([P, P], BF16)
+        eps_col = keep.tile([P, 1], F32)
+        warm = keep.tile([P, 1], F32)
+        sumsq = keep.tile([P, TOK_TILES], F32)
+        rms = keep.tile([P, TOK_TILES], F32)
+        rstd = keep.tile([P, TOK_TILES], F32)
+
+        def load_x(pair):
+            both = slice(2 * pair, 2 * pair + 2)
+            nc.sync.dma_start(out=x_sb[:, both, :], in_=x_rows[:, both, :])
+
+        def load_w(w, c):
+            rows = weights[w][c * K_PASS : (c + 1) * K_PASS, :]
+            nc.sync.dma_start(out=w_raw[w][c][:], in_=rows.rearrange("(p t) n -> p t n", t=PACK))
+
+        def load_vector(v):
+            nc.vector.memset(vec_rows[:, v, :].bitcast(I32), 0)
+            nc.sync.dma_start(out=vec_rows[0:1, v, :], in_=vectors[v].unsqueeze(0))
+
+        nc.vector.memset(eps_col[:], EPS)
+        load_x(0)
+        load_vector(0)
+        load_x(1)
+        load_w(0, 0)
+        load_w(0, 1)
+        for v in range(1, 1 + WEIGHTS):
+            load_vector(v)
+        load_x(2)
+        load_x(3)
+        for w in range(1, WEIGHTS):
+            for c in range(PASSES):
+                load_w(w, c)
+
+        nc.vector.memset(ones[:], 1.0)
+        make_identity(nc, ident[:])
+        nc.scalar.activation(out=warm[:], in_=eps_col[:], func=ACT.Sqrt)
+
+        def spread_vector(engine_copy, v):
+            spread = psum_stage.tile([P, E], BF16, tag="stage")
+            for h in range(N_HALVES):
+                cols = slice(h * N_TILE, (h + 1) * N_TILE)
+                nc.tensor.matmul(
+                    out=spread[:, cols], lhsT=ones[:], rhs=vec_rows[:, v, cols], start=True, stop=True
+                )
+            engine_copy(out=vec_all[:, v, :], in_=spread[:])
+
+        normed = {}
+        transposed = {}
+        grouped_x = {}
+
+        def statistics(pair):
+            both = slice(2 * pair, 2 * pair + 2)
+            for i in range(2 * pair, 2 * pair + 2):
+                squares = work.tile([P, D], BF16, tag="squares")
+                nc.scalar.activation(
+                    out=squares[:], in_=x_sb[:, i, :], func=ACT.Square, accum_out=sumsq[:, i : i + 1]
+                )
+            nc.scalar.activation(
+                out=rms[:, both], in_=sumsq[:, both], func=ACT.Sqrt, scale=1.0 / D, bias=eps_col[:]
+            )
+
+        def normalise(pair):
+            both = slice(2 * pair, 2 * pair + 2)
+            nc.vector.reciprocal(out=rstd[:, both], in_=rms[:, both])
+            for i in range(2 * pair, 2 * pair + 2):
+                xn = work.tile([P, D], BF16, tag="xn")
+                nc.vector.scalar_tensor_tensor(
+                    out=xn[:],
+                    in0=x_sb[:, i, :],
+                    scalar=rstd[:, i : i + 1],
+                    in1=vec_all[:, 0, :],
+                    op0=ALU.mult,
+                    op1=ALU.mult,
+                )
+                normed[i] = xn
+
+        def transpose(pair):
+            for i in range(2 * pair, 2 * pair + 2):
+                xt = psum_stage.tile([P, PASSES, PACK, P], BF16, tag="stage")
+                for c in range(PASSES):
+                    for t in range(PACK):
+                        columns = slice(c * K_PASS + t, (c + 1) * K_PASS, PACK)
+                        nc.tensor.transpose(xt[:, c, t, :], normed[i][:, columns], ident[:])
+                transposed[i] = xt
+
+        def leave_psum(pair):
+            grouped = work.tile([P, 2, PASSES, P, PACK], BF16, tag="grouped_x", align_bytes=64)
+            for half in range(2):
+                xt = transposed[2 * pair + half]
+                nc.scalar.copy(out=grouped[:, half], in_=xt[:].rearrange("p c t r -> p c r t"))
+            grouped_x[pair] = grouped
+
+        def quantise_x(pair):
+            words = slice(2 * pair * TILE_WORDS, (2 * pair + 2) * TILE_WORDS)
+            nc.vector.quantize_mx(
+                out=x_codes[:, words].bitcast(FP8X4),
+                scales=x_scales[:, words],
+                in_=grouped_x[pair][:].rearrange("p a c r t -> p (a c r t)"),
+            )
+
+        grouped_w = {}
+
+        def regroup_w(engine_copy, w, c):
+            grouped = work.tile([P, E * PACK], BF16, tag="grouped_w", align_bytes=64)
+            engine_copy(
+                out=grouped[:].rearrange("p (b i t) -> p b t i", i=4, t=PACK),
+                in_=w_raw[w][c][:].rearrange("p t (b i) -> p b t i", i=4),
+            )
+            grouped_w[(w, c)] = grouped
+
+        def quantise_w(w, c):
+            nc.vector.quantize_mx(
+                out=w_codes[w][:, c, :].bitcast(FP8X4),
+                scales=w_scales[w][:, c, :],
+                in_=grouped_w[(w, c)][:],
+            )
+
+        def project(w, i):
+            result = results.tile([P, E], F32)
+            for h in range(N_HALVES):
+                cols = slice(h * N_TILE, (h + 1) * N_TILE)
+                acc = psum_acc.tile([P, N_TILE], F32)
+                for c in range(PASSES):
+                    words = slice((i * PASSES + c) * P, (i * PASSES + c + 1) * P)
+                    nc.tensor.matmul_mx(
+                        out=acc[:],
+                        lhsT=x_codes[:, words].bitcast(FP8X4),
+                        lhsT_scale=x_scales[:, words],
+                        rhs=w_codes[w][:, c, cols].bitcast(FP8X4),
+                        rhs_scale=w_scales[w][:, c, cols],
+                        start=(c == 0),
+                        stop=(c == PASSES - 1),
+                    )
+                nc.vector.tensor_tensor(
+                    out=result[:, cols], in0=acc[:], in1=vec_all[:, 1 + w, cols], op=ALU.add
+                )
+            nc.sync.dma_start(out=out_rows[w][:, i, :], in_=result[:])
+
+        spread_vector(nc.vector.tensor_copy, 0)
+        for pair in range(LEAD):
+            statistics(pair)
+        for pair in range(LEAD):
+            normalise(pair)
+            transpose(pair)
+            regroup_w(nc.vector.tensor_copy, 0, pair)
+            leave_psum(pair)
+            statistics(pair + LEAD)
+        quantise_w(0, 0)
+        quantise_x(0)
+        quantise_w(0, 1)
+        spread_vector(nc.vector.tensor_copy, 1)
+
+        for w in range(WEIGHTS):
+            for pair in range(PAIRS):
+                if w == 0 and pair + LEAD < PAIRS:
+                    normalise(pair + LEAD)
+                if w + 1 < WEIGHTS:
+                    if pair < PASSES:
+                        regroup_w(nc.scalar.copy, w + 1, pair)
+                    if pair >= PAIRS - PASSES:
+                        quantise_w(w + 1, pair - (PAIRS - PASSES))
+                project(w, 2 * pair)
+                project(w, 2 * pair + 1)
+                if w == 0 and pair + LEAD < PAIRS:
+                    transpose(pair + LEAD)
+                    leave_psum(pair + LEAD)
+                if w == 0 and pair + 1 < PAIRS:
+                    quantise_x(pair + 1)
+                if w + 1 < WEIGHTS and pair == PASSES:
+                    spread_vector(nc.scalar.copy, 2 + w)

@@ -23,16 +23,13 @@ PASSES = D // K_PASS
 TOK_TILES = TOKENS // P
 PAIRS = TOK_TILES // 2
 N_TILE = 512
-N_HALVES = E // N_TILE
+HALVES = E // N_TILE
 WEIGHTS = 3
+CHUNKS = WEIGHTS * HALVES
 TILE_WORDS = PASSES * P
-
-LEAD = 2
+BANK_COLS = 2 * N_TILE // PACK
 
 FLOPS = 2 * TOKENS * D * WEIGHTS * E
-
-assert PAIRS == 2 * LEAD
-assert PASSES == LEAD
 
 
 def tile_tinyblock_pa_kernel(
@@ -40,7 +37,7 @@ def tile_tinyblock_pa_kernel(
 ):
     nc = tc.nc
     weights = [wq, wk, wv]
-    vectors = [attn_norm_w, bq, bk, bv]
+    biases = [bq, bk, bv]
     x_rows = x.flatten_outer_dims().rearrange("(p i) d -> p i d", i=TOK_TILES)
     out_rows = [
         o.flatten_outer_dims().rearrange("(p i) e -> p i e", i=TOK_TILES)
@@ -52,148 +49,204 @@ def tile_tinyblock_pa_kernel(
         keep = ctx.enter_context(tc.tile_pool(name="keep", bufs=1))
         work = ctx.enter_context(tc.tile_pool(name="work", bufs=4))
         results = ctx.enter_context(tc.tile_pool(name="results", bufs=6))
-        psum_stage = ctx.enter_context(tc.psum_pool(name="psum_stage", bufs=3))
-        psum_acc = ctx.enter_context(tc.psum_pool(name="psum_acc", bufs=5))
+        psum_stage = ctx.enter_context(tc.psum_pool(name="psum_stage", bufs=4))
+        psum_acc = ctx.enter_context(tc.psum_pool(name="psum_acc", bufs=4))
 
-        x_sb = keep.tile([P, TOK_TILES, D], BF16)
-        w_raw = [
-            [keep.tile([P, PACK, E], BF16, name="w_raw_%d_%d" % (w, c)) for c in range(PASSES)]
-            for w in range(WEIGHTS)
-        ]
+        x_sb = [keep.tile([P, D], BF16, name="x_sb_%d" % i) for i in range(2)]
+        x_sb += [keep.tile([P, 2, D], BF16, name="x_pair_%d" % k) for k in range(1, PAIRS)]
+        w_raw = {}
+        for h in range(HALVES):
+            for c in range(PASSES):
+                w_raw[(0, h, c)] = keep.tile([P, PACK, N_TILE], BF16, name="w_raw_0_%d_%d" % (h, c))
+        for w in range(1, WEIGHTS):
+            for c in range(PASSES):
+                w_raw[(w, c)] = keep.tile([P, PACK, E], BF16, name="w_raw_%d_%d" % (w, c))
         x_codes = keep.tile([P, TOK_TILES * TILE_WORDS], U32, align_bytes=64)
         x_scales = keep.tile([P, TOK_TILES * TILE_WORDS], U8, align_bytes=64)
         w_codes = [
-            keep.tile([P, PASSES, E], U32, name="w_codes_%d" % w, align_bytes=64)
-            for w in range(WEIGHTS)
+            keep.tile([P, PASSES, N_TILE], U32, name="w_codes_%d" % k, align_bytes=64)
+            for k in range(CHUNKS)
         ]
         w_scales = [
-            keep.tile([P, PASSES, E], U8, name="w_scales_%d" % w, align_bytes=64)
-            for w in range(WEIGHTS)
+            keep.tile([P, PASSES, N_TILE], U8, name="w_scales_%d" % k, align_bytes=64)
+            for k in range(CHUNKS)
         ]
-        vec_rows = keep.tile([P, 1 + WEIGHTS, E], BF16)
-        vec_all = keep.tile([P, 1 + WEIGHTS, E], BF16)
-        ones = keep.tile([P, P], BF16)
-        ident = keep.tile([P, P], BF16)
+        gain_row = keep.tile([P, D], BF16)
+        bias_rows = keep.tile([P, E], BF16)
+        gain_all = keep.tile([P, D], BF16)
+        bias_all = keep.tile([P, WEIGHTS, E], BF16)
+        ident = keep.tile([P, P], F32)
+        ident_bf = keep.tile([P, P], BF16)
         eps_col = keep.tile([P, 1], F32)
         warm = keep.tile([P, 1], F32)
         sumsq = keep.tile([P, TOK_TILES], F32)
-        rms = keep.tile([P, TOK_TILES], F32)
         rstd = keep.tile([P, TOK_TILES], F32)
 
-        def load_x(pair):
-            both = slice(2 * pair, 2 * pair + 2)
-            nc.sync.dma_start(out=x_sb[:, both, :], in_=x_rows[:, both, :])
-
-        def load_w(w, c):
-            rows = weights[w][c * K_PASS : (c + 1) * K_PASS, :]
-            nc.sync.dma_start(out=w_raw[w][c][:], in_=rows.rearrange("(p t) n -> p t n", t=PACK))
-
-        def load_vector(v):
-            nc.vector.memset(vec_rows[:, v, :].bitcast(I32), 0)
-            nc.sync.dma_start(out=vec_rows[0:1, v, :], in_=vectors[v].unsqueeze(0))
+        def x_tile(i):
+            return x_sb[i][:] if i < 2 else x_sb[1 + i // 2][:, i % 2, :]
 
         nc.vector.memset(eps_col[:], EPS)
-        load_x(0)
-        load_vector(0)
+        nc.vector.memset(gain_row[:, : D // 2].bitcast(I32), 0)
+        nc.gpsimd.memset(gain_row[:, D // 2 :].bitcast(I32), 0)
+        make_identity(nc, ident_bf[:])
+        make_identity(nc, ident[:])
+        nc.gpsimd.memset(bias_rows[:].bitcast(I32), 0)
+        nc.scalar.activation(out=warm[:], in_=eps_col[:], func=ACT.Abs_reciprocal_sqrt)
+
+        def load_x(k):
+            if k == 0:
+                for i in range(2):
+                    nc.sync.dma_start(out=x_sb[i][:], in_=x_rows[:, i, :])
+            else:
+                nc.sync.dma_start(out=x_sb[1 + k][:], in_=x_rows[:, 2 * k : 2 * k + 2, :])
+
+        def load_w(w, c, h=None):
+            rows = weights[w][c * K_PASS : (c + 1) * K_PASS, :]
+            if h is None:
+                nc.sync.dma_start(out=w_raw[(w, c)][:], in_=rows.rearrange("(p t) n -> p t n", t=PACK))
+            else:
+                cols = slice(h * N_TILE, (h + 1) * N_TILE)
+                nc.sync.dma_start(
+                    out=w_raw[(w, h, c)][:], in_=rows[:, cols].rearrange("(p t) n -> p t n", t=PACK)
+                )
+
+        nc.sync.dma_start(out=x_sb[0][:], in_=x_rows[:, 0, :])
+        nc.sync.dma_start(out=gain_row[0:1, :], in_=attn_norm_w.unsqueeze(0))
+        nc.sync.dma_start(out=x_sb[1][:], in_=x_rows[:, 1, :])
         load_x(1)
-        load_w(0, 0)
-        load_w(0, 1)
-        for v in range(1, 1 + WEIGHTS):
-            load_vector(v)
+        load_w(0, 0, 0)
+        load_w(0, 1, 0)
+        for v in range(WEIGHTS):
+            nc.sync.dma_start(out=bias_rows[v : v + 1, :], in_=biases[v].unsqueeze(0))
+        load_w(0, 0, 1)
+        load_w(0, 1, 1)
         load_x(2)
         load_x(3)
         for w in range(1, WEIGHTS):
             for c in range(PASSES):
                 load_w(w, c)
 
-        nc.vector.memset(ones[:], 1.0)
-        make_identity(nc, ident[:])
-        nc.scalar.activation(out=warm[:], in_=eps_col[:], func=ACT.Sqrt)
-
-        def spread_vector(engine_copy, v):
+        def spread_vector(rows, v):
             spread = psum_stage.tile([P, E], BF16, tag="stage")
-            for h in range(N_HALVES):
+            for h in range(HALVES):
                 cols = slice(h * N_TILE, (h + 1) * N_TILE)
                 nc.tensor.matmul(
-                    out=spread[:, cols], lhsT=ones[:], rhs=vec_rows[:, v, cols], start=True, stop=True
+                    out=spread[:, cols],
+                    lhsT=ident_bf[:, v : v + 1].to_broadcast([P, P]),
+                    rhs=rows[:, cols],
+                    start=True,
+                    stop=True,
                 )
-            engine_copy(out=vec_all[:, v, :], in_=spread[:])
+            return spread
 
         normed = {}
         transposed = {}
         grouped_x = {}
 
-        def statistics(pair):
-            both = slice(2 * pair, 2 * pair + 2)
-            for i in range(2 * pair, 2 * pair + 2):
-                squares = work.tile([P, D], BF16, tag="squares")
-                nc.scalar.activation(
-                    out=squares[:], in_=x_sb[:, i, :], func=ACT.Square, accum_out=sumsq[:, i : i + 1]
-                )
+        def square_sum(i):
+            squares = work.tile([P, D], BF16, tag="squares")
             nc.scalar.activation(
-                out=rms[:, both], in_=sumsq[:, both], func=ACT.Sqrt, scale=1.0 / D, bias=eps_col[:]
+                out=squares[:], in_=x_tile(i), func=ACT.Square, accum_out=sumsq[:, i : i + 1]
             )
 
-        def normalise(pair):
-            both = slice(2 * pair, 2 * pair + 2)
-            nc.vector.reciprocal(out=rstd[:, both], in_=rms[:, both])
-            for i in range(2 * pair, 2 * pair + 2):
-                xn = work.tile([P, D], BF16, tag="xn")
-                nc.vector.scalar_tensor_tensor(
-                    out=xn[:],
-                    in0=x_sb[:, i, :],
-                    scalar=rstd[:, i : i + 1],
-                    in1=vec_all[:, 0, :],
-                    op0=ALU.mult,
-                    op1=ALU.mult,
-                )
-                normed[i] = xn
+        def inverse_root(sums, first, count):
+            nc.scalar.activation(
+                out=rstd[:, first : first + count],
+                in_=sums,
+                func=ACT.Abs_reciprocal_sqrt,
+                scale=1.0 / D,
+                bias=eps_col[:],
+            )
 
-        def transpose(pair):
-            for i in range(2 * pair, 2 * pair + 2):
-                xt = psum_stage.tile([P, PASSES, PACK, P], BF16, tag="stage")
-                for c in range(PASSES):
-                    for t in range(PACK):
-                        columns = slice(c * K_PASS + t, (c + 1) * K_PASS, PACK)
-                        nc.tensor.transpose(xt[:, c, t, :], normed[i][:, columns], ident[:])
-                transposed[i] = xt
+        def normalise(i):
+            xn = work.tile([P, D], BF16, tag="xn")
+            nc.vector.scalar_tensor_tensor(
+                out=xn[:],
+                in0=x_tile(i),
+                scalar=rstd[:, i : i + 1],
+                in1=gain_all[:],
+                op0=ALU.mult,
+                op1=ALU.mult,
+            )
+            normed[i] = xn
 
-        def leave_psum(pair):
-            grouped = work.tile([P, 2, PASSES, P, PACK], BF16, tag="grouped_x", align_bytes=64)
-            for half in range(2):
-                xt = transposed[2 * pair + half]
-                nc.scalar.copy(out=grouped[:, half], in_=xt[:].rearrange("p c t r -> p c r t"))
-            grouped_x[pair] = grouped
+        def transpose(i):
+            pairs_of_d = normed[i][:].bitcast(F32)
+            xt = psum_stage.tile([P, PASSES, 2, P], F32, tag="stage")
+            for c in range(PASSES):
+                for u in range(2):
+                    columns = slice(c * K_PASS // 2 + u, (c + 1) * K_PASS // 2, 2)
+                    nc.tensor.transpose(xt[:, c, u, :], pairs_of_d[:, columns], ident[:])
+            transposed[i] = xt
 
-        def quantise_x(pair):
-            words = slice(2 * pair * TILE_WORDS, (2 * pair + 2) * TILE_WORDS)
+        def leave_psum(i):
+            k = i // 2
+            if k not in grouped_x:
+                fresh = work.tile([P, 2, PASSES, P, 2], F32, tag="grouped_x", align_bytes=64)
+                grouped_x[k] = fresh
+            nc.scalar.copy(
+                out=grouped_x[k][:, i % 2], in_=transposed[i][:].rearrange("p c u r -> p c r u")
+            )
+
+        def quantise_x(k):
+            words = slice(2 * k * TILE_WORDS, (2 * k + 2) * TILE_WORDS)
             nc.vector.quantize_mx(
                 out=x_codes[:, words].bitcast(FP8X4),
                 scales=x_scales[:, words],
-                in_=grouped_x[pair][:].rearrange("p a c r t -> p (a c r t)"),
+                in_=grouped_x[k][:].rearrange("p a c r u -> p (a c r u)").bitcast(BF16),
             )
 
         grouped_w = {}
 
-        def regroup_w(engine_copy, w, c):
-            grouped = work.tile([P, E * PACK], BF16, tag="grouped_w", align_bytes=64)
+        def raw_of(chunk, c):
+            w, h = divmod(chunk, HALVES)
+            if w == 0:
+                return w_raw[(0, h, c)][:]
+            return w_raw[(w, c)][:, :, h * N_TILE : (h + 1) * N_TILE]
+
+        def regroup_by_copy(engine_copy, chunk, c):
+            grouped = work.tile([P, N_TILE * PACK], BF16, tag="grouped_w", align_bytes=64)
             engine_copy(
                 out=grouped[:].rearrange("p (b i t) -> p b t i", i=4, t=PACK),
-                in_=w_raw[w][c][:].rearrange("p t (b i) -> p b t i", i=4),
+                in_=raw_of(chunk, c).rearrange("p t (b i) -> p b t i", i=4),
             )
-            grouped_w[(w, c)] = grouped
+            grouped_w[(chunk, c)] = grouped
 
-        def quantise_w(w, c):
+        regrouped = {}
+
+        def regroup_on_tensor(chunk, c):
+            raw = raw_of(chunk, c)
+            for b in range(N_TILE // BANK_COLS):
+                bank = psum_stage.tile([P, BANK_COLS * PACK], BF16, tag="stage")
+                for s in range(2):
+                    first = b * BANK_COLS + s * BANK_COLS // 2
+                    nc.tensor.matmul(
+                        out=bank[:, s * N_TILE : (s + 1) * N_TILE],
+                        lhsT=ident_bf[:],
+                        rhs=raw[:, :, first : first + BANK_COLS // 2].rearrange("p t n -> p n t"),
+                        start=True,
+                        stop=True,
+                    )
+                regrouped[(chunk, c, b)] = bank
+
+        def collect(engine_copy, chunk, c):
+            grouped = work.tile([P, N_TILE * PACK], BF16, tag="grouped_w", align_bytes=64)
+            for b in range(N_TILE // BANK_COLS):
+                cols = slice(b * BANK_COLS * PACK, (b + 1) * BANK_COLS * PACK)
+                engine_copy(out=grouped[:, cols], in_=regrouped[(chunk, c, b)][:])
+            grouped_w[(chunk, c)] = grouped
+
+        def quantise_w(chunk, c):
             nc.vector.quantize_mx(
-                out=w_codes[w][:, c, :].bitcast(FP8X4),
-                scales=w_scales[w][:, c, :],
-                in_=grouped_w[(w, c)][:],
+                out=w_codes[chunk][:, c, :].bitcast(FP8X4),
+                scales=w_scales[chunk][:, c, :],
+                in_=grouped_w[(chunk, c)][:],
             )
 
-        def project(w, i):
-            result = results.tile([P, E], F32)
-            for h in range(N_HALVES):
-                cols = slice(h * N_TILE, (h + 1) * N_TILE)
+        accs = {}
+
+        def multiply(chunk, k):
+            for i in range(2 * k, 2 * k + 2):
                 acc = psum_acc.tile([P, N_TILE], F32)
                 for c in range(PASSES):
                     words = slice((i * PASSES + c) * P, (i * PASSES + c + 1) * P)
@@ -201,45 +254,119 @@ def tile_tinyblock_pa_kernel(
                         out=acc[:],
                         lhsT=x_codes[:, words].bitcast(FP8X4),
                         lhsT_scale=x_scales[:, words],
-                        rhs=w_codes[w][:, c, cols].bitcast(FP8X4),
-                        rhs_scale=w_scales[w][:, c, cols],
+                        rhs=w_codes[chunk][:, c, :].bitcast(FP8X4),
+                        rhs_scale=w_scales[chunk][:, c, :],
                         start=(c == 0),
                         stop=(c == PASSES - 1),
                     )
+                accs[(chunk, i)] = acc
+
+        def finish(chunk, k):
+            w, h = divmod(chunk, HALVES)
+            cols = slice(h * N_TILE, (h + 1) * N_TILE)
+            result = results.tile([P, 2, N_TILE], F32)
+            last = chunk == CHUNKS - 1 and k == PAIRS - 1
+            for half in range(2):
+                i = 2 * k + half
                 nc.vector.tensor_tensor(
-                    out=result[:, cols], in0=acc[:], in1=vec_all[:, 1 + w, cols], op=ALU.add
+                    out=result[:, half, :], in0=accs[(chunk, i)][:], in1=bias_all[:, w, cols], op=ALU.add
                 )
-            nc.sync.dma_start(out=out_rows[w][:, i, :], in_=result[:])
+                if last:
+                    nc.sync.dma_start(out=out_rows[w][:, i, cols], in_=result[:, half, :])
+            if not last:
+                nc.sync.dma_start(out=out_rows[w][:, 2 * k : 2 * k + 2, cols], in_=result[:])
 
-        spread_vector(nc.vector.tensor_copy, 0)
-        for pair in range(LEAD):
-            statistics(pair)
-        for pair in range(LEAD):
-            normalise(pair)
-            transpose(pair)
-            regroup_w(nc.vector.tensor_copy, 0, pair)
-            leave_psum(pair)
-            statistics(pair + LEAD)
+        def norm_tile(i):
+            normalise(i)
+
+        def stats(i):
+            square_sum(i)
+            inverse_root(sumsq[:, i : i + 1], i, 1)
+
+        spread = spread_vector(gain_row, 0)
+        nc.vector.tensor_copy(out=gain_all[:], in_=spread[:])
+        stats(0)
+        norm_tile(0)
+        stats(1)
+        norm_tile(1)
+        regroup_on_tensor(0, 0)
+        regroup_on_tensor(0, 1)
+        stats(2)
+        norm_tile(2)
+        transpose(0)
+        transpose(1)
+        collect(nc.scalar.copy, 0, 0)
+        collect(nc.scalar.copy, 0, 1)
+        bias_spread = spread_vector(bias_rows, 0)
+        regroup_on_tensor(1, 0)
         quantise_w(0, 0)
-        quantise_x(0)
         quantise_w(0, 1)
-        spread_vector(nc.vector.tensor_copy, 1)
-
-        for w in range(WEIGHTS):
-            for pair in range(PAIRS):
-                if w == 0 and pair + LEAD < PAIRS:
-                    normalise(pair + LEAD)
-                if w + 1 < WEIGHTS:
-                    if pair < PASSES:
-                        regroup_w(nc.scalar.copy, w + 1, pair)
-                    if pair >= PAIRS - PASSES:
-                        quantise_w(w + 1, pair - (PAIRS - PASSES))
-                project(w, 2 * pair)
-                project(w, 2 * pair + 1)
-                if w == 0 and pair + LEAD < PAIRS:
-                    transpose(pair + LEAD)
-                    leave_psum(pair + LEAD)
-                if w == 0 and pair + 1 < PAIRS:
-                    quantise_x(pair + 1)
-                if w + 1 < WEIGHTS and pair == PASSES:
-                    spread_vector(nc.scalar.copy, 2 + w)
+        leave_psum(0)
+        leave_psum(1)
+        quantise_x(0)
+        multiply(0, 0)
+        regroup_on_tensor(1, 1)
+        transpose(2)
+        stats(3)
+        norm_tile(3)
+        transpose(3)
+        nc.scalar.copy(out=bias_all[:, 0, :], in_=bias_spread[:])
+        finish(0, 0)
+        collect(nc.scalar.copy, 1, 0)
+        collect(nc.scalar.copy, 1, 1)
+        quantise_w(1, 0)
+        quantise_w(1, 1)
+        leave_psum(2)
+        leave_psum(3)
+        multiply(1, 0)
+        quantise_x(1)
+        multiply(0, 1)
+        stats(4)
+        stats(5)
+        stats(6)
+        norm_tile(4)
+        transpose(4)
+        finish(1, 0)
+        norm_tile(5)
+        multiply(1, 1)
+        transpose(5)
+        finish(0, 1)
+        norm_tile(6)
+        transpose(6)
+        leave_psum(4)
+        stats(7)
+        leave_psum(5)
+        quantise_x(2)
+        multiply(0, 2)
+        regroup_by_copy(nc.scalar.copy, 2, 0)
+        leave_psum(6)
+        finish(1, 1)
+        norm_tile(7)
+        transpose(7)
+        multiply(1, 2)
+        regroup_by_copy(nc.scalar.copy, 2, 1)
+        leave_psum(7)
+        finish(0, 2)
+        quantise_w(2, 0)
+        quantise_w(2, 1)
+        quantise_x(3)
+        multiply(0, 3)
+        bias_spread = spread_vector(bias_rows, 1)
+        nc.scalar.copy(out=bias_all[:, 1, :], in_=bias_spread[:])
+        finish(1, 2)
+        multiply(1, 3)
+        finish(0, 3)
+        finish(1, 3)
+        for chunk in range(2, CHUNKS):
+            for k in range(PAIRS):
+                if chunk + 1 < CHUNKS:
+                    if k == 0:
+                        regroup_by_copy(nc.scalar.copy, chunk + 1, 0)
+                        if chunk == 2:
+                            bias_spread = spread_vector(bias_rows, 2)
+                            nc.scalar.copy(out=bias_all[:, 2, :], in_=bias_spread[:])
+                        regroup_by_copy(nc.scalar.copy, chunk + 1, 1)
+                    if k >= 2:
+                        quantise_w(chunk + 1, k - 2)
+                multiply(chunk, k)
+                finish(chunk, k)

@@ -25,9 +25,7 @@ PAIRS = TOK_TILES // 2
 N_TILE = 512
 HALVES = E // N_TILE
 WEIGHTS = 3
-CHUNKS = WEIGHTS * HALVES
 TILE_WORDS = PASSES * P
-BANK_COLS = 2 * N_TILE // PACK
 
 FLOPS = 2 * TOKENS * D * WEIGHTS * E
 
@@ -45,31 +43,28 @@ def tile_tinyblock_pa_kernel(
     ]
 
     with ExitStack() as ctx:
-        ctx.enter_context(tc.manual_schedule())
+        ctx.enter_context(tc.manual_schedule(engines={mybir.EngineType.SP}))
         keep = ctx.enter_context(tc.tile_pool(name="keep", bufs=1))
         work = ctx.enter_context(tc.tile_pool(name="work", bufs=4))
-        results = ctx.enter_context(tc.tile_pool(name="results", bufs=6))
-        psum_stage = ctx.enter_context(tc.psum_pool(name="psum_stage", bufs=4))
-        psum_acc = ctx.enter_context(tc.psum_pool(name="psum_acc", bufs=4))
+        results = ctx.enter_context(tc.tile_pool(name="results", bufs=5))
+        psum_stage = ctx.enter_context(tc.psum_pool(name="psum_stage", bufs=3))
+        psum_acc = ctx.enter_context(tc.psum_pool(name="psum_acc", bufs=5))
 
-        x_sb = [keep.tile([P, D], BF16, name="x_sb_%d" % i) for i in range(2)]
-        x_sb += [keep.tile([P, 2, D], BF16, name="x_pair_%d" % k) for k in range(1, PAIRS)]
-        w_raw = {}
-        for h in range(HALVES):
-            for c in range(PASSES):
-                w_raw[(0, h, c)] = keep.tile([P, PACK, N_TILE], BF16, name="w_raw_0_%d_%d" % (h, c))
-        for w in range(1, WEIGHTS):
-            for c in range(PASSES):
-                w_raw[(w, c)] = keep.tile([P, PACK, E], BF16, name="w_raw_%d_%d" % (w, c))
+        x_head = [keep.tile([P, D], BF16, name="x_head_%d" % i) for i in range(2)]
+        x_pair = [keep.tile([P, 2, D], BF16, name="x_pair_%d" % k) for k in range(1, PAIRS)]
+        w_raw = [
+            [keep.tile([P, PACK, E], BF16, name="w_raw_%d_%d" % (w, c)) for c in range(PASSES)]
+            for w in range(WEIGHTS)
+        ]
         x_codes = keep.tile([P, TOK_TILES * TILE_WORDS], U32, align_bytes=64)
         x_scales = keep.tile([P, TOK_TILES * TILE_WORDS], U8, align_bytes=64)
         w_codes = [
-            keep.tile([P, PASSES, N_TILE], U32, name="w_codes_%d" % k, align_bytes=64)
-            for k in range(CHUNKS)
+            keep.tile([P, HALVES, PASSES, N_TILE], U32, name="w_codes_%d" % w, align_bytes=64)
+            for w in range(WEIGHTS)
         ]
         w_scales = [
-            keep.tile([P, PASSES, N_TILE], U8, name="w_scales_%d" % k, align_bytes=64)
-            for k in range(CHUNKS)
+            keep.tile([P, HALVES, PASSES, N_TILE], U8, name="w_scales_%d" % w, align_bytes=64)
+            for w in range(WEIGHTS)
         ]
         gain_row = keep.tile([P, D], BF16)
         bias_rows = keep.tile([P, E], BF16)
@@ -80,10 +75,11 @@ def tile_tinyblock_pa_kernel(
         eps_col = keep.tile([P, 1], F32)
         warm = keep.tile([P, 1], F32)
         sumsq = keep.tile([P, TOK_TILES], F32)
+        rms = keep.tile([P, TOK_TILES], F32)
         rstd = keep.tile([P, TOK_TILES], F32)
 
         def x_tile(i):
-            return x_sb[i][:] if i < 2 else x_sb[1 + i // 2][:, i % 2, :]
+            return x_head[i][:] if i < 2 else x_pair[i // 2 - 1][:, i % 2, :]
 
         nc.vector.memset(eps_col[:], EPS)
         nc.vector.memset(gain_row[:, : D // 2].bitcast(I32), 0)
@@ -91,37 +87,28 @@ def tile_tinyblock_pa_kernel(
         make_identity(nc, ident_bf[:])
         make_identity(nc, ident[:])
         nc.gpsimd.memset(bias_rows[:].bitcast(I32), 0)
-        nc.scalar.activation(out=warm[:], in_=eps_col[:], func=ACT.Abs_reciprocal_sqrt)
+        nc.scalar.activation(out=warm[:], in_=eps_col[:], func=ACT.Sqrt)
 
-        def load_x(k):
-            if k == 0:
-                for i in range(2):
-                    nc.sync.dma_start(out=x_sb[i][:], in_=x_rows[:, i, :])
-            else:
-                nc.sync.dma_start(out=x_sb[1 + k][:], in_=x_rows[:, 2 * k : 2 * k + 2, :])
+        def load_x_tile(i):
+            nc.sync.dma_start(out=x_head[i][:], in_=x_rows[:, i, :])
 
-        def load_w(w, c, h=None):
+        def load_x_pair(k):
+            nc.sync.dma_start(out=x_pair[k - 1][:], in_=x_rows[:, 2 * k : 2 * k + 2, :])
+
+        def load_w(w, c):
             rows = weights[w][c * K_PASS : (c + 1) * K_PASS, :]
-            if h is None:
-                nc.sync.dma_start(out=w_raw[(w, c)][:], in_=rows.rearrange("(p t) n -> p t n", t=PACK))
-            else:
-                cols = slice(h * N_TILE, (h + 1) * N_TILE)
-                nc.sync.dma_start(
-                    out=w_raw[(w, h, c)][:], in_=rows[:, cols].rearrange("(p t) n -> p t n", t=PACK)
-                )
+            nc.sync.dma_start(out=w_raw[w][c][:], in_=rows.rearrange("(p t) n -> p t n", t=PACK))
 
-        nc.sync.dma_start(out=x_sb[0][:], in_=x_rows[:, 0, :])
+        load_x_tile(0)
         nc.sync.dma_start(out=gain_row[0:1, :], in_=attn_norm_w.unsqueeze(0))
-        nc.sync.dma_start(out=x_sb[1][:], in_=x_rows[:, 1, :])
-        load_x(1)
-        load_w(0, 0, 0)
-        load_w(0, 1, 0)
+        load_x_tile(1)
+        load_w(0, 0)
+        load_x_pair(1)
         for v in range(WEIGHTS):
             nc.sync.dma_start(out=bias_rows[v : v + 1, :], in_=biases[v].unsqueeze(0))
-        load_w(0, 0, 1)
-        load_w(0, 1, 1)
-        load_x(2)
-        load_x(3)
+        load_w(0, 1)
+        load_x_pair(2)
+        load_x_pair(3)
         for w in range(1, WEIGHTS):
             for c in range(PASSES):
                 load_w(w, c)
@@ -143,20 +130,21 @@ def tile_tinyblock_pa_kernel(
         transposed = {}
         grouped_x = {}
 
-        def square_sum(i):
+        def statistics(i):
             squares = work.tile([P, D], BF16, tag="squares")
             nc.scalar.activation(
                 out=squares[:], in_=x_tile(i), func=ACT.Square, accum_out=sumsq[:, i : i + 1]
             )
-
-        def inverse_root(sums, first, count):
             nc.scalar.activation(
-                out=rstd[:, first : first + count],
-                in_=sums,
-                func=ACT.Abs_reciprocal_sqrt,
+                out=rms[:, i : i + 1],
+                in_=sumsq[:, i : i + 1],
+                func=ACT.Sqrt,
                 scale=1.0 / D,
                 bias=eps_col[:],
             )
+
+        def invert(i):
+            nc.vector.reciprocal(out=rstd[:, i : i + 1], in_=rms[:, i : i + 1])
 
         def normalise(i):
             xn = work.tile([P, D], BF16, tag="xn")
@@ -198,175 +186,163 @@ def tile_tinyblock_pa_kernel(
 
         grouped_w = {}
 
-        def raw_of(chunk, c):
-            w, h = divmod(chunk, HALVES)
-            if w == 0:
-                return w_raw[(0, h, c)][:]
-            return w_raw[(w, c)][:, :, h * N_TILE : (h + 1) * N_TILE]
-
-        def regroup_by_copy(engine_copy, chunk, c):
+        def regroup_w(engine_copy, w, h, c):
             grouped = work.tile([P, N_TILE * PACK], BF16, tag="grouped_w", align_bytes=64)
+            cols = slice(h * N_TILE, (h + 1) * N_TILE)
             engine_copy(
                 out=grouped[:].rearrange("p (b i t) -> p b t i", i=4, t=PACK),
-                in_=raw_of(chunk, c).rearrange("p t (b i) -> p b t i", i=4),
+                in_=w_raw[w][c][:, :, cols].rearrange("p t (b i) -> p b t i", i=4),
             )
-            grouped_w[(chunk, c)] = grouped
+            grouped_w[(w, h, c)] = grouped
 
-        regrouped = {}
-
-        def regroup_on_tensor(chunk, c):
-            raw = raw_of(chunk, c)
-            for b in range(N_TILE // BANK_COLS):
-                bank = psum_stage.tile([P, BANK_COLS * PACK], BF16, tag="stage")
-                for s in range(2):
-                    first = b * BANK_COLS + s * BANK_COLS // 2
-                    nc.tensor.matmul(
-                        out=bank[:, s * N_TILE : (s + 1) * N_TILE],
-                        lhsT=ident_bf[:],
-                        rhs=raw[:, :, first : first + BANK_COLS // 2].rearrange("p t n -> p n t"),
-                        start=True,
-                        stop=True,
-                    )
-                regrouped[(chunk, c, b)] = bank
-
-        def collect(engine_copy, chunk, c):
-            grouped = work.tile([P, N_TILE * PACK], BF16, tag="grouped_w", align_bytes=64)
-            for b in range(N_TILE // BANK_COLS):
-                cols = slice(b * BANK_COLS * PACK, (b + 1) * BANK_COLS * PACK)
-                engine_copy(out=grouped[:, cols], in_=regrouped[(chunk, c, b)][:])
-            grouped_w[(chunk, c)] = grouped
-
-        def quantise_w(chunk, c):
+        def quantise_w(w, h, c):
             nc.vector.quantize_mx(
-                out=w_codes[chunk][:, c, :].bitcast(FP8X4),
-                scales=w_scales[chunk][:, c, :],
-                in_=grouped_w[(chunk, c)][:],
+                out=w_codes[w][:, h, c, :].bitcast(FP8X4),
+                scales=w_scales[w][:, h, c, :],
+                in_=grouped_w[(w, h, c)][:],
             )
 
         accs = {}
+        result_of = {}
 
-        def multiply(chunk, k):
-            for i in range(2 * k, 2 * k + 2):
-                acc = psum_acc.tile([P, N_TILE], F32)
-                for c in range(PASSES):
-                    words = slice((i * PASSES + c) * P, (i * PASSES + c + 1) * P)
-                    nc.tensor.matmul_mx(
-                        out=acc[:],
-                        lhsT=x_codes[:, words].bitcast(FP8X4),
-                        lhsT_scale=x_scales[:, words],
-                        rhs=w_codes[chunk][:, c, :].bitcast(FP8X4),
-                        rhs_scale=w_scales[chunk][:, c, :],
-                        start=(c == 0),
-                        stop=(c == PASSES - 1),
-                    )
-                accs[(chunk, i)] = acc
-
-        def finish(chunk, k):
-            w, h = divmod(chunk, HALVES)
-            cols = slice(h * N_TILE, (h + 1) * N_TILE)
-            result = results.tile([P, 2, N_TILE], F32)
-            last = chunk == CHUNKS - 1 and k == PAIRS - 1
-            for half in range(2):
-                i = 2 * k + half
-                nc.vector.tensor_tensor(
-                    out=result[:, half, :], in0=accs[(chunk, i)][:], in1=bias_all[:, w, cols], op=ALU.add
+        def multiply(w, h, i):
+            acc = psum_acc.tile([P, N_TILE], F32)
+            for c in range(PASSES):
+                words = slice((i * PASSES + c) * P, (i * PASSES + c + 1) * P)
+                nc.tensor.matmul_mx(
+                    out=acc[:],
+                    lhsT=x_codes[:, words].bitcast(FP8X4),
+                    lhsT_scale=x_scales[:, words],
+                    rhs=w_codes[w][:, h, c, :].bitcast(FP8X4),
+                    rhs_scale=w_scales[w][:, h, c, :],
+                    start=(c == 0),
+                    stop=(c == PASSES - 1),
                 )
-                if last:
-                    nc.sync.dma_start(out=out_rows[w][:, i, cols], in_=result[:, half, :])
-            if not last:
-                nc.sync.dma_start(out=out_rows[w][:, 2 * k : 2 * k + 2, cols], in_=result[:])
+            accs[(w, h, i)] = acc
 
-        def norm_tile(i):
-            normalise(i)
+        def add_bias(w, h, i):
+            cols = slice(h * N_TILE, (h + 1) * N_TILE)
+            if (w, i) not in result_of:
+                fresh = results.tile([P, E], F32)
+                result_of[(w, i)] = fresh
+            nc.vector.tensor_tensor(
+                out=result_of[(w, i)][:, cols],
+                in0=accs[(w, h, i)][:],
+                in1=bias_all[:, w, cols],
+                op=ALU.add,
+            )
 
-        def stats(i):
-            square_sum(i)
-            inverse_root(sumsq[:, i : i + 1], i, 1)
+        def store(w, i):
+            nc.sync.dma_start(out=out_rows[w][:, i, :], in_=result_of[(w, i)][:])
 
         spread = spread_vector(gain_row, 0)
         nc.vector.tensor_copy(out=gain_all[:], in_=spread[:])
-        stats(0)
-        norm_tile(0)
-        stats(1)
-        norm_tile(1)
-        regroup_on_tensor(0, 0)
-        regroup_on_tensor(0, 1)
-        stats(2)
-        norm_tile(2)
+        statistics(0)
+        invert(0)
+        normalise(0)
+        statistics(1)
+        invert(1)
+        normalise(1)
         transpose(0)
         transpose(1)
-        collect(nc.scalar.copy, 0, 0)
-        collect(nc.scalar.copy, 0, 1)
-        bias_spread = spread_vector(bias_rows, 0)
-        regroup_on_tensor(1, 0)
-        quantise_w(0, 0)
-        quantise_w(0, 1)
+        statistics(2)
+        regroup_w(nc.vector.tensor_copy, 0, 0, 0)
         leave_psum(0)
         leave_psum(1)
+        invert(2)
+        quantise_w(0, 0, 0)
         quantise_x(0)
-        multiply(0, 0)
-        regroup_on_tensor(1, 1)
+        regroup_w(nc.vector.tensor_copy, 0, 0, 1)
+        statistics(3)
+        normalise(2)
         transpose(2)
-        stats(3)
-        norm_tile(3)
+        invert(3)
+        quantise_w(0, 0, 1)
+        normalise(3)
         transpose(3)
-        nc.scalar.copy(out=bias_all[:, 0, :], in_=bias_spread[:])
-        finish(0, 0)
-        collect(nc.scalar.copy, 1, 0)
-        collect(nc.scalar.copy, 1, 1)
-        quantise_w(1, 0)
-        quantise_w(1, 1)
+        regroup_w(nc.scalar.copy, 0, 1, 0)
+        bias_spread = spread_vector(bias_rows, 0)
+        multiply(0, 0, 0)
+        multiply(0, 0, 1)
         leave_psum(2)
         leave_psum(3)
-        multiply(1, 0)
+        nc.scalar.copy(out=bias_all[:, 0, :], in_=bias_spread[:])
+        add_bias(0, 0, 0)
+        add_bias(0, 0, 1)
         quantise_x(1)
-        multiply(0, 1)
-        stats(4)
-        stats(5)
-        stats(6)
-        norm_tile(4)
+        regroup_w(nc.scalar.copy, 0, 1, 1)
+        multiply(0, 0, 2)
+        multiply(0, 0, 3)
+        quantise_w(0, 1, 0)
+        add_bias(0, 0, 2)
+        add_bias(0, 0, 3)
+        quantise_w(0, 1, 1)
+        statistics(4)
+        statistics(5)
+        invert(4)
+        normalise(4)
+        for i in range(4):
+            multiply(0, 1, i)
         transpose(4)
-        finish(1, 0)
-        norm_tile(5)
-        multiply(1, 1)
-        transpose(5)
-        finish(0, 1)
-        norm_tile(6)
-        transpose(6)
         leave_psum(4)
-        stats(7)
+        statistics(6)
+        invert(5)
+        for i in range(2):
+            add_bias(0, 1, i)
+            store(0, i)
+        normalise(5)
+        transpose(5)
         leave_psum(5)
+        statistics(7)
+        invert(6)
+        for i in range(2, 4):
+            add_bias(0, 1, i)
+            store(0, i)
         quantise_x(2)
-        multiply(0, 2)
-        regroup_by_copy(nc.scalar.copy, 2, 0)
-        leave_psum(6)
-        finish(1, 1)
-        norm_tile(7)
+        normalise(6)
+        invert(7)
+        multiply(0, 0, 4)
+        multiply(0, 1, 4)
+        multiply(0, 0, 5)
+        multiply(0, 1, 5)
+        regroup_w(nc.scalar.copy, 1, 0, 0)
+        normalise(7)
+        transpose(6)
         transpose(7)
-        multiply(1, 2)
-        regroup_by_copy(nc.scalar.copy, 2, 1)
+        leave_psum(6)
         leave_psum(7)
-        finish(0, 2)
-        quantise_w(2, 0)
-        quantise_w(2, 1)
+        for i in range(4, 6):
+            for h in range(HALVES):
+                add_bias(0, h, i)
+            store(0, i)
         quantise_x(3)
-        multiply(0, 3)
         bias_spread = spread_vector(bias_rows, 1)
+        regroup_w(nc.scalar.copy, 1, 0, 1)
         nc.scalar.copy(out=bias_all[:, 1, :], in_=bias_spread[:])
-        finish(1, 2)
-        multiply(1, 3)
-        finish(0, 3)
-        finish(1, 3)
-        for chunk in range(2, CHUNKS):
-            for k in range(PAIRS):
-                if chunk + 1 < CHUNKS:
-                    if k == 0:
-                        regroup_by_copy(nc.scalar.copy, chunk + 1, 0)
-                        if chunk == 2:
-                            bias_spread = spread_vector(bias_rows, 2)
-                            nc.scalar.copy(out=bias_all[:, 2, :], in_=bias_spread[:])
-                        regroup_by_copy(nc.scalar.copy, chunk + 1, 1)
-                    if k >= 2:
-                        quantise_w(chunk + 1, k - 2)
-                multiply(chunk, k)
-                finish(chunk, k)
+        quantise_w(1, 0, 0)
+        for i in range(6, 8):
+            for h in range(HALVES):
+                multiply(0, h, i)
+            for h in range(HALVES):
+                add_bias(0, h, i)
+            store(0, i)
+        regroup_w(nc.scalar.copy, 1, 1, 0)
+        regroup_w(nc.scalar.copy, 1, 1, 1)
+        quantise_w(1, 0, 1)
+        bias_spread = spread_vector(bias_rows, 2)
+        nc.scalar.copy(out=bias_all[:, 2, :], in_=bias_spread[:])
+        quantise_w(1, 1, 0)
+        quantise_w(1, 1, 1)
+        for w in range(1, WEIGHTS):
+            for i in range(TOK_TILES):
+                if w + 1 < WEIGHTS and i % 2 == 0:
+                    h, c = divmod(i // 2, PASSES)
+                    regroup_w(nc.scalar.copy, w + 1, h, c)
+                if w + 1 < WEIGHTS and i >= 4:
+                    h, c = divmod(i - 4, PASSES)
+                    quantise_w(w + 1, h, c)
+                for h in range(HALVES):
+                    multiply(w, h, i)
+                for h in range(HALVES):
+                    add_bias(w, h, i)
+                store(w, i)

@@ -43,7 +43,7 @@ def tile_tinyblock_pa_kernel(
     ]
 
     with ExitStack() as ctx:
-        ctx.enter_context(tc.manual_schedule(engines={mybir.EngineType.SP}))
+        ctx.enter_context(tc.manual_schedule())
         keep = ctx.enter_context(tc.tile_pool(name="keep", bufs=1))
         work = ctx.enter_context(tc.tile_pool(name="work", bufs=4))
         results = ctx.enter_context(tc.tile_pool(name="results", bufs=5))
@@ -233,116 +233,130 @@ def tile_tinyblock_pa_kernel(
             )
 
         def store(w, i):
-            nc.sync.dma_start(out=out_rows[w][:, i, :], in_=result_of[(w, i)][:])
+            last = w == WEIGHTS - 1 and i == TOK_TILES - 1
+            width = N_TILE if last else E
+            for first in range(0, E, width):
+                cols = slice(first, first + width)
+                nc.sync.dma_start(out=out_rows[w][:, i, cols], in_=result_of[(w, i)][:, cols])
 
         spread = spread_vector(gain_row, 0)
         nc.vector.tensor_copy(out=gain_all[:], in_=spread[:])
         statistics(0)
+        statistics(1)
         invert(0)
         normalise(0)
-        statistics(1)
         invert(1)
         normalise(1)
         transpose(0)
         transpose(1)
+        regroup_w(nc.scalar.copy, 0, 1, 0)
         statistics(2)
         regroup_w(nc.vector.tensor_copy, 0, 0, 0)
+        quantise_w(0, 0, 0)
+        regroup_w(nc.vector.tensor_copy, 0, 0, 1)
+        invert(2)
         leave_psum(0)
         leave_psum(1)
-        invert(2)
-        quantise_w(0, 0, 0)
-        quantise_x(0)
-        regroup_w(nc.vector.tensor_copy, 0, 0, 1)
         statistics(3)
-        normalise(2)
-        transpose(2)
-        invert(3)
-        quantise_w(0, 0, 1)
-        normalise(3)
-        transpose(3)
-        regroup_w(nc.scalar.copy, 0, 1, 0)
         bias_spread = spread_vector(bias_rows, 0)
+        quantise_x(0)
+        quantise_w(0, 0, 1)
+        normalise(2)
+        nc.scalar.copy(out=bias_all[:, 0, :], in_=bias_spread[:])
+        regroup_w(nc.scalar.copy, 0, 1, 1)
+        invert(3)
         multiply(0, 0, 0)
         multiply(0, 0, 1)
+        transpose(2)
+        normalise(3)
+        transpose(3)
         leave_psum(2)
         leave_psum(3)
-        nc.scalar.copy(out=bias_all[:, 0, :], in_=bias_spread[:])
-        add_bias(0, 0, 0)
-        add_bias(0, 0, 1)
-        quantise_x(1)
-        regroup_w(nc.scalar.copy, 0, 1, 1)
-        multiply(0, 0, 2)
-        multiply(0, 0, 3)
-        quantise_w(0, 1, 0)
-        add_bias(0, 0, 2)
-        add_bias(0, 0, 3)
-        quantise_w(0, 1, 1)
         statistics(4)
         statistics(5)
+        add_bias(0, 0, 0)
+        add_bias(0, 0, 1)
+        quantise_w(0, 1, 0)
+        quantise_w(0, 1, 1)
         invert(4)
+        quantise_x(1)
+        multiply(0, 1, 0)
+        multiply(0, 1, 1)
+        multiply(0, 0, 2)
+        multiply(0, 0, 3)
         normalise(4)
-        for i in range(4):
-            multiply(0, 1, i)
         transpose(4)
-        leave_psum(4)
         statistics(6)
+        leave_psum(4)
         invert(5)
-        for i in range(2):
-            add_bias(0, 1, i)
-            store(0, i)
+        add_bias(0, 1, 0)
+        store(0, 0)
         normalise(5)
         transpose(5)
-        leave_psum(5)
         statistics(7)
+        leave_psum(5)
+        add_bias(0, 1, 1)
+        store(0, 1)
+        multiply(0, 1, 2)
+        multiply(0, 1, 3)
         invert(6)
-        for i in range(2, 4):
-            add_bias(0, 1, i)
-            store(0, i)
-        quantise_x(2)
+        regroup_w(nc.scalar.copy, 1, 0, 0)
+        add_bias(0, 0, 2)
+        add_bias(0, 0, 3)
         normalise(6)
-        invert(7)
+        transpose(6)
+        quantise_x(2)
         multiply(0, 0, 4)
         multiply(0, 1, 4)
+        leave_psum(6)
+        invert(7)
+        add_bias(0, 1, 2)
+        store(0, 2)
+        normalise(7)
+        transpose(7)
+        leave_psum(7)
+        regroup_w(nc.scalar.copy, 1, 0, 1)
+        add_bias(0, 1, 3)
+        store(0, 3)
         multiply(0, 0, 5)
         multiply(0, 1, 5)
-        regroup_w(nc.scalar.copy, 1, 0, 0)
-        normalise(7)
-        transpose(6)
-        transpose(7)
-        leave_psum(6)
-        leave_psum(7)
+        for v in range(1, WEIGHTS):
+            bias_spread = spread_vector(bias_rows, v)
+            nc.scalar.copy(out=bias_all[:, v, :], in_=bias_spread[:])
+        quantise_w(1, 0, 0)
         for i in range(4, 6):
             for h in range(HALVES):
                 add_bias(0, h, i)
             store(0, i)
         quantise_x(3)
-        bias_spread = spread_vector(bias_rows, 1)
-        regroup_w(nc.scalar.copy, 1, 0, 1)
-        nc.scalar.copy(out=bias_all[:, 1, :], in_=bias_spread[:])
-        quantise_w(1, 0, 0)
         for i in range(6, 8):
             for h in range(HALVES):
                 multiply(0, h, i)
-            for h in range(HALVES):
-                add_bias(0, h, i)
-            store(0, i)
         regroup_w(nc.scalar.copy, 1, 1, 0)
         regroup_w(nc.scalar.copy, 1, 1, 1)
         quantise_w(1, 0, 1)
-        bias_spread = spread_vector(bias_rows, 2)
-        nc.scalar.copy(out=bias_all[:, 2, :], in_=bias_spread[:])
+        for h in range(HALVES):
+            add_bias(0, h, 6)
+        store(0, 6)
         quantise_w(1, 1, 0)
+        for h in range(HALVES):
+            add_bias(0, h, 7)
+        store(0, 7)
         quantise_w(1, 1, 1)
         for w in range(1, WEIGHTS):
-            for i in range(TOK_TILES):
-                if w + 1 < WEIGHTS and i % 2 == 0:
+            for i in range(0, TOK_TILES, 2):
+                if w + 1 < WEIGHTS:
                     h, c = divmod(i // 2, PASSES)
                     regroup_w(nc.scalar.copy, w + 1, h, c)
-                if w + 1 < WEIGHTS and i >= 4:
-                    h, c = divmod(i - 4, PASSES)
-                    quantise_w(w + 1, h, c)
                 for h in range(HALVES):
-                    multiply(w, h, i)
+                    for half in range(2):
+                        multiply(w, h, i + half)
+                for half in range(2):
+                    if w + 1 < WEIGHTS and i >= 4:
+                        h, c = divmod(i - 4 + half, PASSES)
+                        quantise_w(w + 1, h, c)
                 for h in range(HALVES):
-                    add_bias(w, h, i)
-                store(w, i)
+                    for half in range(2):
+                        add_bias(w, h, i + half)
+                for half in range(2):
+                    store(w, i + half)

@@ -52,10 +52,19 @@ def tile_tinyblock_pa_kernel(
 
         x_head = [keep.tile([P, D], BF16, name="x_head_%d" % i) for i in range(2)]
         x_pair = [keep.tile([P, 2, D], BF16, name="x_pair_%d" % k) for k in range(1, PAIRS)]
+        w_first = [
+            [keep.tile([P, PACK, N_TILE], BF16, name="w_first_%d_%d" % (h, c)) for c in range(PASSES)]
+            for h in range(HALVES)
+        ]
         w_raw = [
             [keep.tile([P, PACK, E], BF16, name="w_raw_%d_%d" % (w, c)) for c in range(PASSES)]
-            for w in range(WEIGHTS)
+            for w in range(1, WEIGHTS)
         ]
+
+        def raw_quarter(w, h, c):
+            if w == 0:
+                return w_first[h][c][:]
+            return w_raw[w - 1][c][:, :, h * N_TILE : (h + 1) * N_TILE]
         x_codes = keep.tile([P, TOK_TILES * TILE_WORDS], U32, align_bytes=64)
         x_scales = keep.tile([P, TOK_TILES * TILE_WORDS], U8, align_bytes=64)
         w_codes = [
@@ -97,16 +106,22 @@ def tile_tinyblock_pa_kernel(
 
         def load_w(w, c):
             rows = weights[w][c * K_PASS : (c + 1) * K_PASS, :]
-            nc.sync.dma_start(out=w_raw[w][c][:], in_=rows.rearrange("(p t) n -> p t n", t=PACK))
+            nc.sync.dma_start(out=w_raw[w - 1][c][:], in_=rows.rearrange("(p t) n -> p t n", t=PACK))
 
+        def load_first_weight(h, c):
+            rows = wq[c * K_PASS : (c + 1) * K_PASS, h * N_TILE : (h + 1) * N_TILE]
+            nc.sync.dma_start(out=w_first[h][c][:], in_=rows.rearrange("(p t) n -> p t n", t=PACK))
+
+        load_first_weight(0, 0)
         load_x_tile(0)
         nc.sync.dma_start(out=gain_row[0:1, :], in_=attn_norm_w.unsqueeze(0))
         load_x_tile(1)
-        load_w(0, 0)
+        load_first_weight(0, 1)
         load_x_pair(1)
+        load_first_weight(1, 0)
         for v in range(WEIGHTS):
             nc.sync.dma_start(out=bias_rows[v : v + 1, :], in_=biases[v].unsqueeze(0))
-        load_w(0, 1)
+        load_first_weight(1, 1)
         load_x_pair(2)
         load_x_pair(3)
         for w in range(1, WEIGHTS):
@@ -130,21 +145,23 @@ def tile_tinyblock_pa_kernel(
         transposed = {}
         grouped_x = {}
 
-        def statistics(i):
+        def square_sum(i):
             squares = work.tile([P, D], BF16, tag="squares")
             nc.scalar.activation(
                 out=squares[:], in_=x_tile(i), func=ACT.Square, accum_out=sumsq[:, i : i + 1]
             )
+
+        def root(first, end):
             nc.scalar.activation(
-                out=rms[:, i : i + 1],
-                in_=sumsq[:, i : i + 1],
+                out=rms[:, first:end],
+                in_=sumsq[:, first:end],
                 func=ACT.Sqrt,
                 scale=1.0 / D,
                 bias=eps_col[:],
             )
 
-        def invert(i):
-            nc.vector.reciprocal(out=rstd[:, i : i + 1], in_=rms[:, i : i + 1])
+        def invert(first, end):
+            nc.vector.reciprocal(out=rstd[:, first:end], in_=rms[:, first:end])
 
         def normalise(i):
             xn = work.tile([P, D], BF16, tag="xn")
@@ -188,10 +205,9 @@ def tile_tinyblock_pa_kernel(
 
         def regroup_w(engine_copy, w, h, c):
             grouped = work.tile([P, N_TILE * PACK], BF16, tag="grouped_w", align_bytes=64)
-            cols = slice(h * N_TILE, (h + 1) * N_TILE)
             engine_copy(
                 out=grouped[:].rearrange("p (b i t) -> p b t i", i=4, t=PACK),
-                in_=w_raw[w][c][:, :, cols].rearrange("p t (b i) -> p b t i", i=4),
+                in_=raw_quarter(w, h, c).rearrange("p t (b i) -> p b t i", i=4),
             )
             grouped_w[(w, h, c)] = grouped
 
@@ -233,130 +249,133 @@ def tile_tinyblock_pa_kernel(
             )
 
         def store(w, i):
-            last = w == WEIGHTS - 1 and i == TOK_TILES - 1
-            width = N_TILE if last else E
-            for first in range(0, E, width):
-                cols = slice(first, first + width)
-                nc.sync.dma_start(out=out_rows[w][:, i, cols], in_=result_of[(w, i)][:, cols])
+            nc.sync.dma_start(out=out_rows[w][:, i, :], in_=result_of[(w, i)][:])
+
+        def store_half(w, h, i):
+            cols = slice(h * N_TILE, (h + 1) * N_TILE)
+            nc.sync.dma_start(out=out_rows[w][:, i, cols], in_=result_of[(w, i)][:, cols])
 
         spread = spread_vector(gain_row, 0)
-        nc.vector.tensor_copy(out=gain_all[:], in_=spread[:])
-        statistics(0)
-        statistics(1)
-        invert(0)
-        normalise(0)
-        invert(1)
-        normalise(1)
-        transpose(0)
-        transpose(1)
-        regroup_w(nc.scalar.copy, 0, 1, 0)
-        statistics(2)
         regroup_w(nc.vector.tensor_copy, 0, 0, 0)
+        nc.vector.tensor_copy(out=gain_all[:], in_=spread[:])
         quantise_w(0, 0, 0)
+        square_sum(0)
+        root(0, 1)
+        square_sum(1)
+        root(1, 2)
+        invert(0, 1)
+        normalise(0)
+        transpose(0)
+        invert(1, 2)
+        normalise(1)
+        transpose(1)
+        square_sum(2)
         regroup_w(nc.vector.tensor_copy, 0, 0, 1)
-        invert(2)
         leave_psum(0)
+        root(2, 3)
+        square_sum(3)
         leave_psum(1)
-        statistics(3)
+        invert(2, 3)
         bias_spread = spread_vector(bias_rows, 0)
-        quantise_x(0)
+        nc.scalar.copy(out=bias_all[:, 0, :], in_=bias_spread[:])
         quantise_w(0, 0, 1)
         normalise(2)
-        nc.scalar.copy(out=bias_all[:, 0, :], in_=bias_spread[:])
-        regroup_w(nc.scalar.copy, 0, 1, 1)
-        invert(3)
+        quantise_x(0)
+        root(3, 4)
+        invert(3, 4)
         multiply(0, 0, 0)
         multiply(0, 0, 1)
         transpose(2)
         normalise(3)
         transpose(3)
+        regroup_w(nc.scalar.copy, 0, 1, 0)
+        square_sum(4)
         leave_psum(2)
         leave_psum(3)
-        statistics(4)
-        statistics(5)
+        square_sum(5)
         add_bias(0, 0, 0)
         add_bias(0, 0, 1)
+        regroup_w(nc.vector.tensor_copy, 0, 1, 1)
         quantise_w(0, 1, 0)
-        quantise_w(0, 1, 1)
-        invert(4)
         quantise_x(1)
-        multiply(0, 1, 0)
-        multiply(0, 1, 1)
-        multiply(0, 0, 2)
-        multiply(0, 0, 3)
+        quantise_w(0, 1, 1)
+        root(4, 6)
+        for i in range(2):
+            multiply(0, 1, i)
+        for i in range(2, 4):
+            multiply(0, 0, i)
+        square_sum(6)
+        square_sum(7)
+        root(6, 8)
+        regroup_w(nc.scalar.copy, 1, 0, 0)
+        invert(4, 6)
         normalise(4)
         transpose(4)
-        statistics(6)
-        leave_psum(4)
-        invert(5)
         add_bias(0, 1, 0)
         store(0, 0)
         normalise(5)
         transpose(5)
-        statistics(7)
-        leave_psum(5)
         add_bias(0, 1, 1)
         store(0, 1)
-        multiply(0, 1, 2)
-        multiply(0, 1, 3)
-        invert(6)
-        regroup_w(nc.scalar.copy, 1, 0, 0)
+        leave_psum(4)
+        leave_psum(5)
+        for i in range(2, 4):
+            multiply(0, 1, i)
         add_bias(0, 0, 2)
+        invert(6, 8)
         add_bias(0, 0, 3)
         normalise(6)
         transpose(6)
         quantise_x(2)
-        multiply(0, 0, 4)
-        multiply(0, 1, 4)
-        leave_psum(6)
-        invert(7)
-        add_bias(0, 1, 2)
-        store(0, 2)
+        regroup_w(nc.scalar.copy, 1, 0, 1)
         normalise(7)
         transpose(7)
+        leave_psum(6)
         leave_psum(7)
-        regroup_w(nc.scalar.copy, 1, 0, 1)
-        add_bias(0, 1, 3)
-        store(0, 3)
-        multiply(0, 0, 5)
-        multiply(0, 1, 5)
+        for i in range(4, 6):
+            for h in range(HALVES):
+                multiply(0, h, i)
+        for i in range(2, 4):
+            add_bias(0, 1, i)
+            store(0, i)
+        quantise_w(1, 0, 0)
+        quantise_x(3)
+        regroup_w(nc.scalar.copy, 1, 1, 0)
         for v in range(1, WEIGHTS):
             bias_spread = spread_vector(bias_rows, v)
             nc.scalar.copy(out=bias_all[:, v, :], in_=bias_spread[:])
-        quantise_w(1, 0, 0)
+        for i in range(6, 8):
+            for h in range(HALVES):
+                multiply(0, h, i)
+        regroup_w(nc.scalar.copy, 1, 1, 1)
         for i in range(4, 6):
             for h in range(HALVES):
                 add_bias(0, h, i)
             store(0, i)
-        quantise_x(3)
+        quantise_w(1, 0, 1)
         for i in range(6, 8):
             for h in range(HALVES):
-                multiply(0, h, i)
-        regroup_w(nc.scalar.copy, 1, 1, 0)
-        regroup_w(nc.scalar.copy, 1, 1, 1)
-        quantise_w(1, 0, 1)
-        for h in range(HALVES):
-            add_bias(0, h, 6)
-        store(0, 6)
+                add_bias(0, h, i)
+            store(0, i)
         quantise_w(1, 1, 0)
-        for h in range(HALVES):
-            add_bias(0, h, 7)
-        store(0, 7)
         quantise_w(1, 1, 1)
         for w in range(1, WEIGHTS):
             for i in range(0, TOK_TILES, 2):
                 if w + 1 < WEIGHTS:
                     h, c = divmod(i // 2, PASSES)
                     regroup_w(nc.scalar.copy, w + 1, h, c)
-                for h in range(HALVES):
-                    for half in range(2):
-                        multiply(w, h, i + half)
-                for half in range(2):
+                by_half = [(h, i + j) for h in range(HALVES) for j in range(2)]
+                by_tile = [(h, i + j) for j in range(2) for h in range(HALVES)]
+                parts = by_half if (w, i) == (1, 0) else by_tile
+                for h, j in parts:
+                    multiply(w, h, j)
+                for j in range(2):
                     if w + 1 < WEIGHTS and i >= 4:
-                        h, c = divmod(i - 4 + half, PASSES)
+                        h, c = divmod(i - 4 + j, PASSES)
                         quantise_w(w + 1, h, c)
-                for h in range(HALVES):
-                    for half in range(2):
-                        add_bias(w, h, i + half)
-                for half in range(2):
-                    store(w, i + half)
+                for h, j in parts:
+                    add_bias(w, h, j)
+                    if w + 1 == WEIGHTS and j + 1 == TOK_TILES:
+                        store_half(w, h, j)
+                    elif h + 1 == HALVES:
+                        store(w, j)

@@ -81,22 +81,24 @@ def tile_tinyblock_pa_kernel(
         bias_all = keep.tile([P, WEIGHTS, E], BF16)
         ident = keep.tile([P, P], F32)
         ident_bf = keep.tile([P, P], BF16)
-        eps_col = keep.tile([P, 1], F32)
+        zero_col = keep.tile([P, 1], F32)
         warm = keep.tile([P, 1], F32)
         sumsq = keep.tile([P, TOK_TILES], F32)
-        rms = keep.tile([P, TOK_TILES], F32)
+        mean_square = keep.tile([P, TOK_TILES], F32)
+        minus_half = keep.tile([P, TOK_TILES], F32)
         rstd = keep.tile([P, TOK_TILES], F32)
 
         def x_tile(i):
             return x_head[i][:] if i < 2 else x_pair[i // 2 - 1][:, i % 2, :]
 
-        nc.vector.memset(eps_col[:], EPS)
+        nc.vector.memset(zero_col[:], 0.0)
+        nc.vector.memset(minus_half[:], -0.5)
         nc.vector.memset(gain_row[:, : D // 2].bitcast(I32), 0)
         nc.gpsimd.memset(gain_row[:, D // 2 :].bitcast(I32), 0)
         make_identity(nc, ident_bf[:])
         make_identity(nc, ident[:])
         nc.gpsimd.memset(bias_rows[:].bitcast(I32), 0)
-        nc.scalar.activation(out=warm[:], in_=eps_col[:], func=ACT.Sqrt)
+        nc.scalar.activation(out=warm[:], in_=zero_col[:], func=ACT.Square)
 
         def load_x_tile(i):
             nc.sync.dma_start(out=x_head[i][:], in_=x_rows[:, i, :])
@@ -113,11 +115,11 @@ def tile_tinyblock_pa_kernel(
             nc.sync.dma_start(out=w_first[h][c][:], in_=rows.rearrange("(p t) n -> p t n", t=PACK))
 
         load_first_weight(0, 0)
-        load_x_tile(0)
         nc.sync.dma_start(out=gain_row[0:1, :], in_=attn_norm_w.unsqueeze(0))
+        load_x_tile(0)
         load_x_tile(1)
-        load_first_weight(0, 1)
         load_x_pair(1)
+        load_first_weight(0, 1)
         load_first_weight(1, 0)
         for v in range(WEIGHTS):
             nc.sync.dma_start(out=bias_rows[v : v + 1, :], in_=biases[v].unsqueeze(0))
@@ -151,17 +153,19 @@ def tile_tinyblock_pa_kernel(
                 out=squares[:], in_=x_tile(i), func=ACT.Square, accum_out=sumsq[:, i : i + 1]
             )
 
-        def root(first, end):
-            nc.scalar.activation(
-                out=rms[:, first:end],
-                in_=sumsq[:, first:end],
-                func=ACT.Sqrt,
-                scale=1.0 / D,
-                bias=eps_col[:],
+        def inverse_rms(first, end):
+            tiles = slice(first, end)
+            nc.gpsimd.tensor_scalar(
+                out=mean_square[:, tiles],
+                in0=sumsq[:, tiles],
+                scalar1=1.0 / D,
+                scalar2=EPS,
+                op0=ALU.mult,
+                op1=ALU.add,
             )
-
-        def invert(first, end):
-            nc.vector.reciprocal(out=rstd[:, first:end], in_=rms[:, first:end])
+            nc.gpsimd.tensor_tensor(
+                out=rstd[:, tiles], in0=mean_square[:, tiles], in1=minus_half[:, tiles], op=ALU.pow
+            )
 
         def normalise(i):
             xn = work.tile([P, D], BF16, tag="xn")
@@ -260,55 +264,51 @@ def tile_tinyblock_pa_kernel(
         nc.vector.tensor_copy(out=gain_all[:], in_=spread[:])
         quantise_w(0, 0, 0)
         square_sum(0)
-        root(0, 1)
+        inverse_rms(0, 1)
         square_sum(1)
-        root(1, 2)
-        invert(0, 1)
+        inverse_rms(1, 2)
         normalise(0)
         transpose(0)
-        invert(1, 2)
+        bias_spread = spread_vector(bias_rows, 0)
         normalise(1)
         transpose(1)
         square_sum(2)
+        inverse_rms(2, 3)
         regroup_w(nc.vector.tensor_copy, 0, 0, 1)
-        leave_psum(0)
-        root(2, 3)
         square_sum(3)
-        leave_psum(1)
-        invert(2, 3)
-        bias_spread = spread_vector(bias_rows, 0)
+        inverse_rms(3, 4)
+        leave_psum(0)
         nc.scalar.copy(out=bias_all[:, 0, :], in_=bias_spread[:])
-        quantise_w(0, 0, 1)
+        leave_psum(1)
         normalise(2)
+        quantise_w(0, 0, 1)
         quantise_x(0)
-        root(3, 4)
-        invert(3, 4)
+        normalise(3)
         multiply(0, 0, 0)
         multiply(0, 0, 1)
         transpose(2)
-        normalise(3)
         transpose(3)
         regroup_w(nc.scalar.copy, 0, 1, 0)
         square_sum(4)
+        inverse_rms(4, 5)
         leave_psum(2)
         leave_psum(3)
         square_sum(5)
+        inverse_rms(5, 6)
+        regroup_w(nc.vector.tensor_copy, 0, 1, 1)
         add_bias(0, 0, 0)
         add_bias(0, 0, 1)
-        regroup_w(nc.vector.tensor_copy, 0, 1, 1)
         quantise_w(0, 1, 0)
         quantise_x(1)
         quantise_w(0, 1, 1)
-        root(4, 6)
         for i in range(2):
             multiply(0, 1, i)
         for i in range(2, 4):
             multiply(0, 0, i)
         square_sum(6)
         square_sum(7)
-        root(6, 8)
+        inverse_rms(6, 8)
         regroup_w(nc.scalar.copy, 1, 0, 0)
-        invert(4, 6)
         normalise(4)
         transpose(4)
         add_bias(0, 1, 0)
@@ -322,36 +322,38 @@ def tile_tinyblock_pa_kernel(
         for i in range(2, 4):
             multiply(0, 1, i)
         add_bias(0, 0, 2)
-        invert(6, 8)
         add_bias(0, 0, 3)
         normalise(6)
         transpose(6)
         quantise_x(2)
+        for h in range(HALVES):
+            multiply(0, h, 4)
         regroup_w(nc.scalar.copy, 1, 0, 1)
         normalise(7)
         transpose(7)
         leave_psum(6)
         leave_psum(7)
-        for i in range(4, 6):
-            for h in range(HALVES):
-                multiply(0, h, i)
+        for h in range(HALVES):
+            multiply(0, h, 5)
         for i in range(2, 4):
             add_bias(0, 1, i)
             store(0, i)
         quantise_w(1, 0, 0)
-        quantise_x(3)
         regroup_w(nc.scalar.copy, 1, 1, 0)
         for v in range(1, WEIGHTS):
             bias_spread = spread_vector(bias_rows, v)
             nc.scalar.copy(out=bias_all[:, v, :], in_=bias_spread[:])
+        regroup_w(nc.scalar.copy, 1, 1, 1)
+        for h in range(HALVES):
+            add_bias(0, h, 4)
+        store(0, 4)
+        quantise_x(3)
         for i in range(6, 8):
             for h in range(HALVES):
                 multiply(0, h, i)
-        regroup_w(nc.scalar.copy, 1, 1, 1)
-        for i in range(4, 6):
-            for h in range(HALVES):
-                add_bias(0, h, i)
-            store(0, i)
+        for h in range(HALVES):
+            add_bias(0, h, 5)
+        store(0, 5)
         quantise_w(1, 0, 1)
         for i in range(6, 8):
             for h in range(HALVES):

@@ -81,24 +81,22 @@ def tile_tinyblock_pa_kernel(
         bias_all = keep.tile([P, WEIGHTS, E], BF16)
         ident = keep.tile([P, P], F32)
         ident_bf = keep.tile([P, P], BF16)
-        zero_col = keep.tile([P, 1], F32)
+        eps_col = keep.tile([P, 1], F32)
         warm = keep.tile([P, 1], F32)
         sumsq = keep.tile([P, TOK_TILES], F32)
-        mean_square = keep.tile([P, TOK_TILES], F32)
-        minus_half = keep.tile([P, TOK_TILES], F32)
+        rms = keep.tile([P, TOK_TILES], F32)
         rstd = keep.tile([P, TOK_TILES], F32)
 
         def x_tile(i):
             return x_head[i][:] if i < 2 else x_pair[i // 2 - 1][:, i % 2, :]
 
-        nc.vector.memset(zero_col[:], 0.0)
-        nc.vector.memset(minus_half[:], -0.5)
+        nc.vector.memset(eps_col[:], EPS)
         nc.vector.memset(gain_row[:, : D // 2].bitcast(I32), 0)
         nc.gpsimd.memset(gain_row[:, D // 2 :].bitcast(I32), 0)
         make_identity(nc, ident_bf[:])
         make_identity(nc, ident[:])
         nc.gpsimd.memset(bias_rows[:].bitcast(I32), 0)
-        nc.scalar.activation(out=warm[:], in_=zero_col[:], func=ACT.Square)
+        nc.scalar.activation(out=warm[:], in_=eps_col[:], func=ACT.Sqrt)
 
         def load_x_tile(i):
             nc.sync.dma_start(out=x_head[i][:], in_=x_rows[:, i, :])
@@ -153,19 +151,17 @@ def tile_tinyblock_pa_kernel(
                 out=squares[:], in_=x_tile(i), func=ACT.Square, accum_out=sumsq[:, i : i + 1]
             )
 
-        def inverse_rms(first, end):
-            tiles = slice(first, end)
-            nc.gpsimd.tensor_scalar(
-                out=mean_square[:, tiles],
-                in0=sumsq[:, tiles],
-                scalar1=1.0 / D,
-                scalar2=EPS,
-                op0=ALU.mult,
-                op1=ALU.add,
+        def root(first, end):
+            nc.scalar.activation(
+                out=rms[:, first:end],
+                in_=sumsq[:, first:end],
+                func=ACT.Sqrt,
+                scale=1.0 / D,
+                bias=eps_col[:],
             )
-            nc.gpsimd.tensor_tensor(
-                out=rstd[:, tiles], in0=mean_square[:, tiles], in1=minus_half[:, tiles], op=ALU.pow
-            )
+
+        def invert(first, end):
+            nc.vector.reciprocal(out=rstd[:, first:end], in_=rms[:, first:end])
 
         def normalise(i):
             xn = work.tile([P, D], BF16, tag="xn")
@@ -264,24 +260,26 @@ def tile_tinyblock_pa_kernel(
         nc.vector.tensor_copy(out=gain_all[:], in_=spread[:])
         quantise_w(0, 0, 0)
         square_sum(0)
-        inverse_rms(0, 1)
+        root(0, 1)
         square_sum(1)
-        inverse_rms(1, 2)
+        root(1, 2)
+        invert(0, 1)
         normalise(0)
         transpose(0)
         bias_spread = spread_vector(bias_rows, 0)
+        invert(1, 2)
         normalise(1)
         transpose(1)
         square_sum(2)
-        inverse_rms(2, 3)
         regroup_w(nc.vector.tensor_copy, 0, 0, 1)
         square_sum(3)
-        inverse_rms(3, 4)
         leave_psum(0)
+        root(2, 4)
         nc.scalar.copy(out=bias_all[:, 0, :], in_=bias_spread[:])
         leave_psum(1)
-        normalise(2)
+        invert(2, 4)
         quantise_w(0, 0, 1)
+        normalise(2)
         quantise_x(0)
         normalise(3)
         multiply(0, 0, 0)
@@ -290,27 +288,30 @@ def tile_tinyblock_pa_kernel(
         transpose(3)
         regroup_w(nc.scalar.copy, 0, 1, 0)
         square_sum(4)
-        inverse_rms(4, 5)
         leave_psum(2)
+        root(4, 5)
         leave_psum(3)
         square_sum(5)
-        inverse_rms(5, 6)
         regroup_w(nc.vector.tensor_copy, 0, 1, 1)
         add_bias(0, 0, 0)
         add_bias(0, 0, 1)
         quantise_w(0, 1, 0)
         quantise_x(1)
+        invert(4, 5)
         quantise_w(0, 1, 1)
         for i in range(2):
             multiply(0, 1, i)
         for i in range(2, 4):
             multiply(0, 0, i)
         square_sum(6)
+        root(5, 6)
         square_sum(7)
-        inverse_rms(6, 8)
+        root(6, 7)
         regroup_w(nc.scalar.copy, 1, 0, 0)
+        root(7, 8)
         normalise(4)
         transpose(4)
+        invert(5, 6)
         add_bias(0, 1, 0)
         store(0, 0)
         normalise(5)
@@ -322,9 +323,11 @@ def tile_tinyblock_pa_kernel(
         for i in range(2, 4):
             multiply(0, 1, i)
         add_bias(0, 0, 2)
+        invert(6, 7)
         add_bias(0, 0, 3)
         normalise(6)
         transpose(6)
+        invert(7, 8)
         quantise_x(2)
         for h in range(HALVES):
             multiply(0, h, 4)

@@ -25,6 +25,8 @@ PAIRS = TOK_TILES // 2
 N_TILE = 512
 HALVES = E // N_TILE
 WEIGHTS = 3
+TAIL = [N_TILE, N_TILE // 2]
+LEAD = N_TILE // 2
 TILE_WORDS = PASSES * P
 
 FLOPS = 2 * TOKENS * D * WEIGHTS * E
@@ -47,8 +49,9 @@ def tile_tinyblock_pa_kernel(
         keep = ctx.enter_context(tc.tile_pool(name="keep", bufs=1))
         work = ctx.enter_context(tc.tile_pool(name="work", bufs=4))
         results = ctx.enter_context(tc.tile_pool(name="results", bufs=5))
+        psum_gain = ctx.enter_context(tc.psum_pool(name="psum_gain", bufs=1))
         psum_stage = ctx.enter_context(tc.psum_pool(name="psum_stage", bufs=3))
-        psum_acc = ctx.enter_context(tc.psum_pool(name="psum_acc", bufs=5))
+        psum_acc = ctx.enter_context(tc.psum_pool(name="psum_acc", bufs=4))
 
         x_head = [keep.tile([P, D], BF16, name="x_head_%d" % i) for i in range(2)]
         x_pair = [keep.tile([P, 2, D], BF16, name="x_pair_%d" % k) for k in range(1, PAIRS)]
@@ -61,7 +64,11 @@ def tile_tinyblock_pa_kernel(
             for w in range(1, WEIGHTS)
         ]
 
-        def raw_quarter(w, h, c):
+        w_lead = [keep.tile([P, PACK, LEAD], BF16, name="w_lead_%d" % b) for b in range(2)]
+
+        def raw_columns(w, h, c, first, width):
+            if (w, h, c) == (0, 0, 0):
+                return w_lead[first // LEAD][:]
             if w == 0:
                 return w_first[h][c][:]
             return w_raw[w - 1][c][:, :, h * N_TILE : (h + 1) * N_TILE]
@@ -77,7 +84,6 @@ def tile_tinyblock_pa_kernel(
         ]
         gain_row = keep.tile([P, D], BF16)
         bias_rows = keep.tile([P, E], BF16)
-        gain_all = keep.tile([P, D], BF16)
         bias_all = keep.tile([P, WEIGHTS, E], BF16)
         ident = keep.tile([P, P], F32)
         ident_bf = keep.tile([P, P], BF16)
@@ -108,13 +114,18 @@ def tile_tinyblock_pa_kernel(
             rows = weights[w][c * K_PASS : (c + 1) * K_PASS, :]
             nc.sync.dma_start(out=w_raw[w - 1][c][:], in_=rows.rearrange("(p t) n -> p t n", t=PACK))
 
+        def load_lead(b):
+            rows = wq[:K_PASS, b * LEAD : (b + 1) * LEAD]
+            nc.sync.dma_start(out=w_lead[b][:], in_=rows.rearrange("(p t) n -> p t n", t=PACK))
+
         def load_first_weight(h, c):
             rows = wq[c * K_PASS : (c + 1) * K_PASS, h * N_TILE : (h + 1) * N_TILE]
             nc.sync.dma_start(out=w_first[h][c][:], in_=rows.rearrange("(p t) n -> p t n", t=PACK))
 
-        load_first_weight(0, 0)
-        nc.sync.dma_start(out=gain_row[0:1, :], in_=attn_norm_w.unsqueeze(0))
+        load_lead(0)
         load_x_tile(0)
+        nc.sync.dma_start(out=gain_row[0:1, :], in_=attn_norm_w.unsqueeze(0))
+        load_lead(1)
         load_x_tile(1)
         load_x_pair(1)
         load_first_weight(0, 1)
@@ -128,8 +139,7 @@ def tile_tinyblock_pa_kernel(
             for c in range(PASSES):
                 load_w(w, c)
 
-        def spread_vector(rows, v):
-            spread = psum_stage.tile([P, E], BF16, tag="stage")
+        def spread_vector(spread, rows, v):
             for h in range(HALVES):
                 cols = slice(h * N_TILE, (h + 1) * N_TILE)
                 nc.tensor.matmul(
@@ -139,7 +149,15 @@ def tile_tinyblock_pa_kernel(
                     start=True,
                     stop=True,
                 )
-            return spread
+
+        bias_spread = {}
+
+        def spread_bias(v):
+            bias_spread[v] = psum_stage.tile([P, E], BF16, tag="stage", name="bias_spread")
+            spread_vector(bias_spread[v], bias_rows, v)
+
+        def collect_bias(v):
+            nc.scalar.copy(out=bias_all[:, v, :], in_=bias_spread[v][:])
 
         normed = {}
         transposed = {}
@@ -203,19 +221,22 @@ def tile_tinyblock_pa_kernel(
 
         grouped_w = {}
 
-        def regroup_w(engine_copy, w, h, c):
-            grouped = work.tile([P, N_TILE * PACK], BF16, tag="grouped_w", align_bytes=64)
+        def regroup_w(engine_copy, w, h, c, first=0, width=N_TILE):
+            if first == 0:
+                fresh = work.tile([P, N_TILE * PACK], BF16, tag="grouped_w", align_bytes=64)
+                grouped_w[(w, h, c)] = fresh
+            grouped = grouped_w[(w, h, c)][:, first * PACK : (first + width) * PACK]
             engine_copy(
-                out=grouped[:].rearrange("p (b i t) -> p b t i", i=4, t=PACK),
-                in_=raw_quarter(w, h, c).rearrange("p t (b i) -> p b t i", i=4),
+                out=grouped.rearrange("p (b i t) -> p b t i", i=4, t=PACK),
+                in_=raw_columns(w, h, c, first, width).rearrange("p t (b i) -> p b t i", i=4),
             )
-            grouped_w[(w, h, c)] = grouped
 
-        def quantise_w(w, h, c):
+        def quantise_w(w, h, c, first=0, width=N_TILE):
+            cols = slice(first, first + width)
             nc.vector.quantize_mx(
-                out=w_codes[w][:, h, c, :].bitcast(FP8X4),
-                scales=w_scales[w][:, h, c, :],
-                in_=grouped_w[(w, h, c)][:],
+                out=w_codes[w][:, h, c, cols].bitcast(FP8X4),
+                scales=w_scales[w][:, h, c, cols],
+                in_=grouped_w[(w, h, c)][:, first * PACK : (first + width) * PACK],
             )
 
         accs = {}
@@ -236,14 +257,14 @@ def tile_tinyblock_pa_kernel(
                 )
             accs[(w, h, i)] = acc
 
-        def add_bias(w, h, i):
-            cols = slice(h * N_TILE, (h + 1) * N_TILE)
+        def add_bias(w, h, i, first=0, width=N_TILE):
+            cols = slice(h * N_TILE + first, h * N_TILE + first + width)
             if (w, i) not in result_of:
                 fresh = results.tile([P, E], F32)
                 result_of[(w, i)] = fresh
             nc.vector.tensor_tensor(
                 out=result_of[(w, i)][:, cols],
-                in0=accs[(w, h, i)][:],
+                in0=accs[(w, h, i)][:, first : first + width],
                 in1=bias_all[:, w, cols],
                 op=ALU.add,
             )
@@ -251,22 +272,24 @@ def tile_tinyblock_pa_kernel(
         def store(w, i):
             nc.sync.dma_start(out=out_rows[w][:, i, :], in_=result_of[(w, i)][:])
 
-        def store_half(w, h, i):
-            cols = slice(h * N_TILE, (h + 1) * N_TILE)
+        def store_part(w, h, i, first, width):
+            cols = slice(h * N_TILE + first, h * N_TILE + first + width)
             nc.sync.dma_start(out=out_rows[w][:, i, cols], in_=result_of[(w, i)][:, cols])
 
-        spread = spread_vector(gain_row, 0)
-        regroup_w(nc.vector.tensor_copy, 0, 0, 0)
-        nc.vector.tensor_copy(out=gain_all[:], in_=spread[:])
-        quantise_w(0, 0, 0)
+        gain_all = psum_gain.tile([P, D], BF16)
+        spread_vector(gain_all, gain_row, 0)
+        for b in range(2):
+            regroup_w(nc.vector.tensor_copy, 0, 0, 0, b * LEAD, LEAD)
         square_sum(0)
         root(0, 1)
         square_sum(1)
         root(1, 2)
+        quantise_w(0, 0, 0, 0, LEAD)
         invert(0, 1)
+        quantise_w(0, 0, 0, LEAD, LEAD)
         normalise(0)
         transpose(0)
-        bias_spread = spread_vector(bias_rows, 0)
+        spread_bias(0)
         invert(1, 2)
         normalise(1)
         transpose(1)
@@ -275,7 +298,7 @@ def tile_tinyblock_pa_kernel(
         square_sum(3)
         leave_psum(0)
         root(2, 4)
-        nc.scalar.copy(out=bias_all[:, 0, :], in_=bias_spread[:])
+        collect_bias(0)
         leave_psum(1)
         invert(2, 4)
         quantise_w(0, 0, 1)
@@ -344,8 +367,8 @@ def tile_tinyblock_pa_kernel(
         quantise_w(1, 0, 0)
         regroup_w(nc.scalar.copy, 1, 1, 0)
         for v in range(1, WEIGHTS):
-            bias_spread = spread_vector(bias_rows, v)
-            nc.scalar.copy(out=bias_all[:, v, :], in_=bias_spread[:])
+            spread_bias(v)
+        collect_bias(1)
         regroup_w(nc.scalar.copy, 1, 1, 1)
         for h in range(HALVES):
             add_bias(0, h, 4)
@@ -364,6 +387,7 @@ def tile_tinyblock_pa_kernel(
             store(0, i)
         quantise_w(1, 1, 0)
         quantise_w(1, 1, 1)
+        after_tile = {3: [(0, 0)], 4: [(0, 1)], 5: [(1, 0)], 6: [(1, 1)]}
         for w in range(1, WEIGHTS):
             for i in range(0, TOK_TILES, 2):
                 if w + 1 < WEIGHTS:
@@ -374,13 +398,17 @@ def tile_tinyblock_pa_kernel(
                 parts = by_half if (w, i) == (1, 0) else by_tile
                 for h, j in parts:
                     multiply(w, h, j)
-                for j in range(2):
-                    if w + 1 < WEIGHTS and i >= 4:
-                        h, c = divmod(i - 4 + j, PASSES)
-                        quantise_w(w + 1, h, c)
+                if w == 1 and i == 0:
+                    collect_bias(2)
                 for h, j in parts:
-                    add_bias(w, h, j)
                     if w + 1 == WEIGHTS and j + 1 == TOK_TILES:
-                        store_half(w, h, j)
-                    elif h + 1 == HALVES:
+                        for first in range(0, N_TILE, TAIL[h]):
+                            add_bias(w, h, j, first, TAIL[h])
+                            store_part(w, h, j, first, TAIL[h])
+                        continue
+                    add_bias(w, h, j)
+                    if h + 1 == HALVES:
                         store(w, j)
+                        if w + 1 < WEIGHTS:
+                            for hh, c in after_tile.get(j, []):
+                                quantise_w(w + 1, hh, c)

@@ -25,7 +25,6 @@ PAIRS = TOK_TILES // 2
 N_TILE = 512
 HALVES = E // N_TILE
 WEIGHTS = 3
-TAIL = [N_TILE, N_TILE // 2]
 LEAD = N_TILE // 2
 TILE_WORDS = PASSES * P
 
@@ -257,24 +256,20 @@ def tile_tinyblock_pa_kernel(
                 )
             accs[(w, h, i)] = acc
 
-        def add_bias(w, h, i, first=0, width=N_TILE):
-            cols = slice(h * N_TILE + first, h * N_TILE + first + width)
+        def add_bias(w, h, i):
+            cols = slice(h * N_TILE, (h + 1) * N_TILE)
             if (w, i) not in result_of:
                 fresh = results.tile([P, E], F32)
                 result_of[(w, i)] = fresh
             nc.vector.tensor_tensor(
                 out=result_of[(w, i)][:, cols],
-                in0=accs[(w, h, i)][:, first : first + width],
+                in0=accs[(w, h, i)][:],
                 in1=bias_all[:, w, cols],
                 op=ALU.add,
             )
 
         def store(w, i):
             nc.sync.dma_start(out=out_rows[w][:, i, :], in_=result_of[(w, i)][:])
-
-        def store_part(w, h, i, first, width):
-            cols = slice(h * N_TILE + first, h * N_TILE + first + width)
-            nc.sync.dma_start(out=out_rows[w][:, i, cols], in_=result_of[(w, i)][:, cols])
 
         gain_all = psum_gain.tile([P, D], BF16)
         spread_vector(gain_all, gain_row, 0)
@@ -387,7 +382,6 @@ def tile_tinyblock_pa_kernel(
             store(0, i)
         quantise_w(1, 1, 0)
         quantise_w(1, 1, 1)
-        after_tile = {3: [(0, 0)], 4: [(0, 1)], 5: [(1, 0)], 6: [(1, 1)]}
         for w in range(1, WEIGHTS):
             for i in range(0, TOK_TILES, 2):
                 if w + 1 < WEIGHTS:
@@ -398,17 +392,11 @@ def tile_tinyblock_pa_kernel(
                 parts = by_half if (w, i) == (1, 0) else by_tile
                 for h, j in parts:
                     multiply(w, h, j)
-                if w == 1 and i == 0:
+                if (w, i) == (1, 0):
                     collect_bias(2)
                 for h, j in parts:
-                    if w + 1 == WEIGHTS and j + 1 == TOK_TILES:
-                        for first in range(0, N_TILE, TAIL[h]):
-                            add_bias(w, h, j, first, TAIL[h])
-                            store_part(w, h, j, first, TAIL[h])
-                        continue
                     add_bias(w, h, j)
                     if h + 1 == HALVES:
                         store(w, j)
-                        if w + 1 < WEIGHTS:
-                            for hh, c in after_tile.get(j, []):
-                                quantise_w(w + 1, hh, c)
+                        if w + 1 < WEIGHTS and 3 <= j <= 6:
+                            quantise_w(w + 1, (j - 3) // PASSES, (j - 3) % PASSES)

@@ -47,10 +47,9 @@ def tile_tinyblock_pa_kernel(
         ctx.enter_context(tc.manual_schedule())
         keep = ctx.enter_context(tc.tile_pool(name="keep", bufs=1))
         work = ctx.enter_context(tc.tile_pool(name="work", bufs=4))
-        results = ctx.enter_context(tc.tile_pool(name="results", bufs=5))
-        psum_gain = ctx.enter_context(tc.psum_pool(name="psum_gain", bufs=1))
+        results = ctx.enter_context(tc.tile_pool(name="results", bufs=12))
         psum_stage = ctx.enter_context(tc.psum_pool(name="psum_stage", bufs=3))
-        psum_acc = ctx.enter_context(tc.psum_pool(name="psum_acc", bufs=4))
+        psum_acc = ctx.enter_context(tc.psum_pool(name="psum_acc", bufs=5))
 
         x_head = [keep.tile([P, D], BF16, name="x_head_%d" % i) for i in range(2)]
         x_pair = [keep.tile([P, 2, D], BF16, name="x_pair_%d" % k) for k in range(1, PAIRS)]
@@ -83,6 +82,7 @@ def tile_tinyblock_pa_kernel(
         ]
         gain_row = keep.tile([P, D], BF16)
         bias_rows = keep.tile([P, E], BF16)
+        gain_all = keep.tile([P, D], BF16)
         bias_all = keep.tile([P, WEIGHTS, E], BF16)
         ident = keep.tile([P, P], F32)
         ident_bf = keep.tile([P, P], BF16)
@@ -271,21 +271,22 @@ def tile_tinyblock_pa_kernel(
         def store(w, i):
             nc.sync.dma_start(out=out_rows[w][:, i, :], in_=result_of[(w, i)][:])
 
-        gain_all = psum_gain.tile([P, D], BF16)
-        spread_vector(gain_all, gain_row, 0)
+        gain_spread = psum_stage.tile([P, D], BF16, tag="stage")
+        spread_vector(gain_spread, gain_row, 0)
         for b in range(2):
             regroup_w(nc.vector.tensor_copy, 0, 0, 0, b * LEAD, LEAD)
+        nc.vector.tensor_copy(out=gain_all[:], in_=gain_spread[:])
         square_sum(0)
         root(0, 1)
         square_sum(1)
         root(1, 2)
-        quantise_w(0, 0, 0, 0, LEAD)
         invert(0, 1)
-        quantise_w(0, 0, 0, LEAD, LEAD)
+        quantise_w(0, 0, 0, 0, LEAD)
         normalise(0)
         transpose(0)
         spread_bias(0)
         invert(1, 2)
+        quantise_w(0, 0, 0, LEAD, LEAD)
         normalise(1)
         transpose(1)
         square_sum(2)

from contextlib import ExitStack

import concourse.mybir as mybir
from concourse.masks import make_identity

F32 = mybir.dt.float32
BF16 = mybir.dt.bfloat16
I32 = mybir.dt.int32
U32 = mybir.dt.uint32
U8 = mybir.dt.uint8
FP8X4 = mybir.dt.float8_e4m3fn_x4
ACT = mybir.ActivationFunctionType
ALU = mybir.AluOpType

P = 128
PACK = 4
K_PASS = P * PACK
TOKENS = 4 * 256
D = 1024
E = 1024
EPS = 1e-6
PASSES = D // K_PASS
TOK_TILES = TOKENS // P
PAIRS = TOK_TILES // 2
N_TILE = 512
HALVES = E // N_TILE
WEIGHTS = 3
LEAD = N_TILE // 2
TILE_WORDS = PASSES * P

FLOPS = 2 * TOKENS * D * WEIGHTS * E


def tile_tinyblock_pa_kernel(
    tc, x, attn_norm_w, wq, bq, wk, bk, wv, bv, out_0, out_1, out_2
):
    nc = tc.nc
    weights = [wq, wk, wv]
    biases = [bq, bk, bv]
    x_rows = x.flatten_outer_dims().rearrange("(p i) d -> p i d", i=TOK_TILES)
    out_rows = [
        o.flatten_outer_dims().rearrange("(p i) e -> p i e", i=TOK_TILES)
        for o in (out_0, out_1, out_2)
    ]

    with ExitStack() as ctx:
        ctx.enter_context(tc.manual_schedule())
        keep = ctx.enter_context(tc.tile_pool(name="keep", bufs=1))
        work = ctx.enter_context(tc.tile_pool(name="work", bufs=4))
        results = ctx.enter_context(tc.tile_pool(name="results", bufs=12))
        psum_stage = ctx.enter_context(tc.psum_pool(name="psum_stage", bufs=3))
        psum_acc = ctx.enter_context(tc.psum_pool(name="psum_acc", bufs=5))

        x_head = [keep.tile([P, D], BF16, name="x_head_%d" % i) for i in range(2)]
        x_pair = [keep.tile([P, 2, D], BF16, name="x_pair_%d" % k) for k in range(1, PAIRS)]
        w_first = [
            [keep.tile([P, PACK, N_TILE], BF16, name="w_first_%d_%d" % (h, c)) for c in range(PASSES)]
            for h in range(HALVES)
        ]
        w_raw = [
            [keep.tile([P, PACK, E], BF16, name="w_raw_%d_%d" % (w, c)) for c in range(PASSES)]
            for w in range(1, WEIGHTS)
        ]

        w_lead = [keep.tile([P, PACK, LEAD], BF16, name="w_lead_%d" % b) for b in range(2)]

        def raw_columns(w, h, c, first, width):
            if (w, h, c) == (0, 0, 0):
                return w_lead[first // LEAD][:]
            if w == 0:
                return w_first[h][c][:]
            return w_raw[w - 1][c][:, :, h * N_TILE : (h + 1) * N_TILE]
        x_codes = keep.tile([P, TOK_TILES * TILE_WORDS], U32, align_bytes=64)
        x_scales = keep.tile([P, TOK_TILES * TILE_WORDS], U8, align_bytes=64)
        w_codes = [
            keep.tile([P, HALVES, PASSES, N_TILE], U32, name="w_codes_%d" % w, align_bytes=64)
            for w in range(WEIGHTS)
        ]
        w_scales = [
            keep.tile([P, HALVES, PASSES, N_TILE], U8, name="w_scales_%d" % w, align_bytes=64)
            for w in range(WEIGHTS)
        ]
        gain_row = keep.tile([P, D], BF16)
        bias_rows = keep.tile([P, E], BF16)
        gain_all = keep.tile([P, D], BF16)
        bias_all = keep.tile([P, WEIGHTS, E], BF16)
        ident = keep.tile([P, P], F32)
        ident_bf = keep.tile([P, P], BF16)
        eps_col = keep.tile([P, 1], F32)
        warm = keep.tile([P, 1], F32)
        sumsq = keep.tile([P, TOK_TILES], F32)
        rms = keep.tile([P, TOK_TILES], F32)
        rstd = keep.tile([P, TOK_TILES], F32)

        def x_tile(i):
            return x_head[i][:] if i < 2 else x_pair[i // 2 - 1][:, i % 2, :]

        nc.vector.memset(eps_col[:], EPS)
        nc.vector.memset(gain_row[:, : D // 2].bitcast(I32), 0)
        nc.gpsimd.memset(gain_row[:, D // 2 :].bitcast(I32), 0)
        make_identity(nc, ident_bf[:])
        make_identity(nc, ident[:])
        nc.gpsimd.memset(bias_rows[:].bitcast(I32), 0)
        nc.scalar.activation(out=warm[:], in_=eps_col[:], func=ACT.Sqrt)

        def load_x_tile(i):
            nc.sync.dma_start(out=x_head[i][:], in_=x_rows[:, i, :])

        def load_x_pair(k):
            nc.sync.dma_start(out=x_pair[k - 1][:], in_=x_rows[:, 2 * k : 2 * k + 2, :])

        def load_w(w, c):
            rows = weights[w][c * K_PASS : (c + 1) * K_PASS, :]
            nc.sync.dma_start(out=w_raw[w - 1][c][:], in_=rows.rearrange("(p t) n -> p t n", t=PACK))

        def load_lead(b):
            rows = wq[:K_PASS, b * LEAD : (b + 1) * LEAD]
            nc.sync.dma_start(out=w_lead[b][:], in_=rows.rearrange("(p t) n -> p t n", t=PACK))

        def load_first_weight(h, c):
            rows = wq[c * K_PASS : (c + 1) * K_PASS, h * N_TILE : (h + 1) * N_TILE]
            nc.sync.dma_start(out=w_first[h][c][:], in_=rows.rearrange("(p t) n -> p t n", t=PACK))

        load_lead(0)
        load_x_tile(0)
        nc.sync.dma_start(out=gain_row[0:1, :], in_=attn_norm_w.unsqueeze(0))
        load_lead(1)
        load_x_tile(1)
        load_x_pair(1)
        load_first_weight(0, 1)
        load_first_weight(1, 0)
        for v in range(WEIGHTS):
            nc.sync.dma_start(out=bias_rows[v : v + 1, :], in_=biases[v].unsqueeze(0))
        load_first_weight(1, 1)
        load_x_pair(2)
        load_x_pair(3)
        for w in range(1, WEIGHTS):
            for c in range(PASSES):
                load_w(w, c)

        def spread_vector(spread, rows, v):
            for h in range(HALVES):
                cols = slice(h * N_TILE, (h + 1) * N_TILE)
                nc.tensor.matmul(
                    out=spread[:, cols],
                    lhsT=ident_bf[:, v : v + 1].to_broadcast([P, P]),
                    rhs=rows[:, cols],
                    start=True,
                    stop=True,
                )

        bias_spread = {}

        def spread_bias(v):
            bias_spread[v] = psum_stage.tile([P, E], BF16, tag="stage", name="bias_spread")
            spread_vector(bias_spread[v], bias_rows, v)

        def collect_bias(v):
            nc.scalar.copy(out=bias_all[:, v, :], in_=bias_spread[v][:])

        normed = {}
        transposed = {}
        grouped_x = {}

        def square_sum(i):
            squares = work.tile([P, D], BF16, tag="squares")
            nc.scalar.activation(
                out=squares[:], in_=x_tile(i), func=ACT.Square, accum_out=sumsq[:, i : i + 1]
            )

        def root(first, end):
            nc.scalar.activation(
                out=rms[:, first:end],
                in_=sumsq[:, first:end],
                func=ACT.Sqrt,
                scale=1.0 / D,
                bias=eps_col[:],
            )

        def invert(first, end):
            nc.vector.reciprocal(out=rstd[:, first:end], in_=rms[:, first:end])

        def normalise(i):
            xn = work.tile([P, D], BF16, tag="xn")
            nc.vector.scalar_tensor_tensor(
                out=xn[:],
                in0=x_tile(i),
                scalar=rstd[:, i : i + 1],
                in1=gain_all[:],
                op0=ALU.mult,
                op1=ALU.mult,
            )
            normed[i] = xn

        def transpose(i):
            pairs_of_d = normed[i][:].bitcast(F32)
            xt = psum_stage.tile([P, PASSES, 2, P], F32, tag="stage")
            for c in range(PASSES):
                for u in range(2):
                    columns = slice(c * K_PASS // 2 + u, (c + 1) * K_PASS // 2, 2)
                    nc.tensor.transpose(xt[:, c, u, :], pairs_of_d[:, columns], ident[:])
            transposed[i] = xt

        def leave_psum(i):
            k = i // 2
            if k not in grouped_x:
                fresh = work.tile([P, 2, PASSES, P, 2], F32, tag="grouped_x", align_bytes=64)
                grouped_x[k] = fresh
            nc.scalar.copy(
                out=grouped_x[k][:, i % 2], in_=transposed[i][:].rearrange("p c u r -> p c r u")
            )

        def quantise_x(k):
            words = slice(2 * k * TILE_WORDS, (2 * k + 2) * TILE_WORDS)
            nc.vector.quantize_mx(
                out=x_codes[:, words].bitcast(FP8X4),
                scales=x_scales[:, words],
                in_=grouped_x[k][:].rearrange("p a c r u -> p (a c r u)").bitcast(BF16),
            )

        grouped_w = {}

        def regroup_w(engine_copy, w, h, c, first=0, width=N_TILE):
            if first == 0:
                fresh = work.tile([P, N_TILE * PACK], BF16, tag="grouped_w", align_bytes=64)
                grouped_w[(w, h, c)] = fresh
            grouped = grouped_w[(w, h, c)][:, first * PACK : (first + width) * PACK]
            engine_copy(
                out=grouped.rearrange("p (b i t) -> p b t i", i=4, t=PACK),
                in_=raw_columns(w, h, c, first, width).rearrange("p t (b i) -> p b t i", i=4),
            )

        def quantise_w(w, h, c, first=0, width=N_TILE):
            cols = slice(first, first + width)
            nc.vector.quantize_mx(
                out=w_codes[w][:, h, c, cols].bitcast(FP8X4),
                scales=w_scales[w][:, h, c, cols],
                in_=grouped_w[(w, h, c)][:, first * PACK : (first + width) * PACK],
            )

        accs = {}
        result_of = {}

        def multiply(w, h, i):
            acc = psum_acc.tile([P, N_TILE], F32)
            for c in range(PASSES):
                words = slice((i * PASSES + c) * P, (i * PASSES + c + 1) * P)
                nc.tensor.matmul_mx(
                    out=acc[:],
                    lhsT=x_codes[:, words].bitcast(FP8X4),
                    lhsT_scale=x_scales[:, words],
                    rhs=w_codes[w][:, h, c, :].bitcast(FP8X4),
                    rhs_scale=w_scales[w][:, h, c, :],
                    start=(c == 0),
                    stop=(c == PASSES - 1),
                )
            accs[(w, h, i)] = acc

        def add_bias(w, h, i):
            cols = slice(h * N_TILE, (h + 1) * N_TILE)
            if (w, i) not in result_of:
                fresh = results.tile([P, E], F32)
                result_of[(w, i)] = fresh
            nc.vector.tensor_tensor(
                out=result_of[(w, i)][:, cols],
                in0=accs[(w, h, i)][:],
                in1=bias_all[:, w, cols],
                op=ALU.add,
            )

        def store(w, i):
            nc.sync.dma_start(out=out_rows[w][:, i, :], in_=result_of[(w, i)][:])

        gain_spread = psum_stage.tile([P, D], BF16, tag="stage")
        spread_vector(gain_spread, gain_row, 0)
        for b in range(2):
            regroup_w(nc.vector.tensor_copy, 0, 0, 0, b * LEAD, LEAD)
        nc.vector.tensor_copy(out=gain_all[:], in_=gain_spread[:])
        square_sum(0)
        root(0, 1)
        square_sum(1)
        root(1, 2)
        invert(0, 1)
        quantise_w(0, 0, 0, 0, LEAD)
        normalise(0)
        transpose(0)
        spread_bias(0)
        invert(1, 2)
        quantise_w(0, 0, 0, LEAD, LEAD)
        normalise(1)
        transpose(1)
        square_sum(2)
        regroup_w(nc.vector.tensor_copy, 0, 0, 1)
        square_sum(3)
        leave_psum(0)
        root(2, 4)
        collect_bias(0)
        leave_psum(1)
        invert(2, 4)
        quantise_w(0, 0, 1)
        normalise(2)
        quantise_x(0)
        normalise(3)
        multiply(0, 0, 0)
        multiply(0, 0, 1)
        transpose(2)
        transpose(3)
        regroup_w(nc.scalar.copy, 0, 1, 0)
        square_sum(4)
        leave_psum(2)
        root(4, 5)
        leave_psum(3)
        square_sum(5)
        regroup_w(nc.vector.tensor_copy, 0, 1, 1)
        add_bias(0, 0, 0)
        add_bias(0, 0, 1)
        quantise_w(0, 1, 0)
        quantise_x(1)
        invert(4, 5)
        quantise_w(0, 1, 1)
        for i in range(2):
            multiply(0, 1, i)
        for i in range(2, 4):
            multiply(0, 0, i)
        square_sum(6)
        root(5, 6)
        square_sum(7)
        root(6, 7)
        regroup_w(nc.scalar.copy, 1, 0, 0)
        root(7, 8)
        normalise(4)
        transpose(4)
        invert(5, 6)
        add_bias(0, 1, 0)
        store(0, 0)
        normalise(5)
        transpose(5)
        add_bias(0, 1, 1)
        store(0, 1)
        leave_psum(4)
        leave_psum(5)
        for i in range(2, 4):
            multiply(0, 1, i)
        add_bias(0, 0, 2)
        invert(6, 7)
        add_bias(0, 0, 3)
        normalise(6)
        transpose(6)
        invert(7, 8)
        quantise_x(2)
        for h in range(HALVES):
            multiply(0, h, 4)
        regroup_w(nc.scalar.copy, 1, 0, 1)
        normalise(7)
        transpose(7)
        leave_psum(6)
        leave_psum(7)
        for h in range(HALVES):
            multiply(0, h, 5)
        for i in range(2, 4):
            add_bias(0, 1, i)
            store(0, i)
        quantise_w(1, 0, 0)
        regroup_w(nc.scalar.copy, 1, 1, 0)
        for v in range(1, WEIGHTS):
            spread_bias(v)
        collect_bias(1)
        regroup_w(nc.scalar.copy, 1, 1, 1)
        for h in range(HALVES):
            add_bias(0, h, 4)
        store(0, 4)
        quantise_x(3)
        for i in range(6, 8):
            for h in range(HALVES):
                multiply(0, h, i)
        for h in range(HALVES):
            add_bias(0, h, 5)
        store(0, 5)
        quantise_w(1, 0, 1)
        for i in range(6, 8):
            for h in range(HALVES):
                add_bias(0, h, i)
            store(0, i)
        quantise_w(1, 1, 0)
        quantise_w(1, 1, 1)
        for w in range(1, WEIGHTS):
            for i in range(0, TOK_TILES, 2):
                if w + 1 < WEIGHTS:
                    h, c = divmod(i // 2, PASSES)
                    regroup_w(nc.scalar.copy, w + 1, h, c)
                by_half = [(h, i + j) for h in range(HALVES) for j in range(2)]
                by_tile = [(h, i + j) for j in range(2) for h in range(HALVES)]
                parts = by_half if (w, i) == (1, 0) else by_tile
                for h, j in parts:
                    multiply(w, h, j)
                if (w, i) == (1, 0):
                    collect_bias(2)
                for h, j in parts:
                    add_bias(w, h, j)
                    if h + 1 == HALVES:
                        store(w, j)
                        if w + 1 < WEIGHTS and 3 <= j <= 6:
                            quantise_w(w + 1, (j - 3) // PASSES, (j - 3) % PASSES)
